import numpy as np
import ml_dtypes


def mxq(x, axis, fmt="e4m3"):
    dtype, down = {"e4m3": (ml_dtypes.float8_e4m3fn, 7), "e5m2": (ml_dtypes.float8_e5m2, 14)}[fmt]
    v = np.moveaxis(np.asarray(x, np.float32).astype(ml_dtypes.bfloat16).astype(np.float64), axis, -1)
    blocks = v.reshape(v.shape[:-1] + (-1, 32))
    amax = np.abs(blocks).max(-1, keepdims=True)
    byte = np.maximum(np.where(amax > 0, np.frexp(amax)[1] - 1 + 127, 0) - down, 1)
    scale = np.exp2(byte - 127.0)
    codes = (blocks / scale).astype(np.float32).astype(dtype).astype(np.float64)
    return np.moveaxis((codes * scale).reshape(v.shape), -1, axis)


WIDE = False


def mx_kscale(k):
    if not WIDE:
        return np.ones(k)
    levels = np.array([10, -10, 5, -5, 0])
    a = np.random.permutation(np.resize(levels, k // 512 * 4)).reshape(k // 512, 4)
    idx = np.arange(k)
    return np.exp2(a[idx // 512, idx % 128 // 32])


BF16 = ml_dtypes.bfloat16


def bf(x):
    return np.asarray(x, np.float32).astype(BF16)


def f64(x):
    return np.asarray(x).astype(np.float64)


N, E, DIM = 1024, 4096, 512
DENSITY = 0.005
BARE = 0.02


def draw_incidence():
    inc = np.random.random((N, E)) < DENSITY
    inc[np.random.random(N) < BARE, :] = False
    inc[:, np.random.random(E) < BARE] = False
    return bf(inc)


def setup_inputs():
    t = mx_kscale(DIM)
    return {
        "x_0_local": bf(np.random.standard_normal((N, DIM)) * t),
        "x_1_new": bf(np.random.standard_normal((E, DIM)) * 1.3),
        "incidence_1": draw_incidence(),
        "Wr": bf(np.random.standard_normal((DIM, DIM)) * 2.0 / np.sqrt(DIM) / t[:, None]),
        "br": bf(np.random.standard_normal(DIM) * 0.3),
        "gate_return": bf(0.8 + 0.4 * np.random.random(1)),
    }


def reference(x_0_local, x_1_new, incidence_1, Wr, br, gate_return):
    H = f64(incidence_1)
    D_v = np.maximum(H.sum(1, keepdims=True), 1.0)
    D_e = np.maximum(H.sum(0, keepdims=True), 1.0)
    H_norm = H / np.sqrt(D_v) / np.sqrt(D_e)
    ret_msg = mxq(H_norm.T, 1, "e4m3") @ mxq(f64(x_0_local), 0, "e4m3")
    upd = (mxq(ret_msg, 1, "e4m3") @ mxq(f64(Wr), 0, "e4m3")) + f64(br)
    return f64(x_1_new) + np.tanh(f64(gate_return)) * upd

@@ -1,0 +1,262 @@
+from contextlib import ExitStack
+
+import concourse.bass as bass
+import concourse.mybir as mybir
+import concourse.tile as tile
+from concourse.masks import make_identity
+
+F32 = mybir.dt.float32
+BF16 = mybir.dt.bfloat16
+U32 = mybir.dt.uint32
+U8 = mybir.dt.uint8
+FP8X4 = mybir.dt.float8_e4m3fn_x4
+ALU = mybir.AluOpType
+ACT = mybir.ActivationFunctionType
+AX = mybir.AxisListType
+
+P = 128
+N_NODES = 1024
+E = 4096
+DIM = 512
+PLANES = 8
+CH = 512
+ROUNDS = E // CH
+SUB = CH // P
+
+FLOPS = 2 * E * N_NODES * DIM + 2 * E * DIM * DIM
+
+
+def tile_hypergraphgpslayer_pb_t_kernel(
+    tc, x_0_local, x_1_new, incidence_1, Wr, br, gate_return, out
+):
+    nc = tc.nc
+    with ExitStack() as ctx:
+        const = ctx.enter_context(tc.tile_pool(name="const", bufs=1))
+        tt_pool = ctx.enter_context(tc.tile_pool(name="tt", bufs=3))
+        hg_pool = ctx.enter_context(tc.tile_pool(name="hg", bufs=2))
+        hq_pool = ctx.enter_context(tc.tile_pool(name="hq", bufs=2))
+        rg_pool = ctx.enter_context(tc.tile_pool(name="rg", bufs=2))
+        x1_pool = ctx.enter_context(tc.tile_pool(name="x1", bufs=3))
+        ob_pool = ctx.enter_context(tc.tile_pool(name="ob", bufs=3))
+        pa = ctx.enter_context(tc.psum_pool(name="pa", bufs=4))
+        pb = ctx.enter_context(tc.psum_pool(name="pb", bufs=4))
+
+        gate_b = const.tile([P, 1], BF16)
+        nc.sync.dma_start(out=gate_b[:], in_=gate_return.partition_broadcast(P))
+
+        h_raw = const.tile([P, PLANES, E], BF16)
+        h_dram = incidence_1.rearrange("(g p j) e -> p g j e", g=2, j=4)
+        pieces = [(a, 0, E) for a in range(PLANES - 1)] + [
+            (PLANES - 1, 0, E // 2),
+            (PLANES - 1, E // 2, E // 2),
+        ]
+        for a, c0, n in pieces:
+            nc.sync.dma_start(out=h_raw[:, a, c0 : c0 + n], in_=h_dram[:, a // 4, a % 4, c0 : c0 + n])
+
+        x0raw = const.tile([P, 2, 4, DIM], BF16)
+        nc.sync.dma_start(
+            out=x0raw[:], in_=x_0_local.rearrange("(g p j) d -> p g j d", g=2, j=4)
+        )
+        wraw = const.tile([P, 4, DIM], BF16)
+        nc.sync.dma_start(out=wraw[:], in_=Wr.rearrange("(p t) o -> p t o", t=4))
+        br_b = const.tile([P, DIM], BF16)
+        nc.sync.dma_start(out=br_b[:], in_=br.partition_broadcast(P))
+
+        ident = const.tile([P, P], F32)
+        make_identity(nc, ident[:])
+        ones = const.tile([P, 2], BF16)
+        nc.vector.memset(ones[:], 1.0)
+        dv_v = const.tile([P, PLANES, 2], F32)
+        nc.vector.memset(dv_v[:], 0.0)
+        dv_s = const.tile([P, PLANES], F32)
+        nc.vector.memset(dv_s[:], 0.0)
+
+        g_col = const.tile([P, 1], F32)
+        nc.scalar.activation(out=g_col[:], in_=gate_b[:], func=ACT.Tanh)
+        warm = const.tile([P, 1], F32)
+        nc.scalar.activation(out=warm[:], in_=g_col[:], func=ACT.Sqrt, bias=1.0, scale=0.0)
+
+        s_tasks = [(0, 0, 4096), (2, 0, 4096), (4, 0, 2048), (6, 2048, 2048), (7, 3072, 1024)]
+        v_tasks = [
+            (1, 0, 4096, 0),
+            (3, 0, 4096, 0),
+            (4, 2048, 2048, 0),
+            (5, 0, 4096, 0),
+            (6, 0, 2048, 0),
+            (7, 0, 2048, 0),
+            (7, 2048, 1024, 1),
+        ]
+        for a, c0, n in s_tasks:
+            junk_s = tt_pool.tile([P, PLANES, CH], BF16, tag="tt")
+            nc.scalar.activation(
+                out=junk_s[:].rearrange("p a e -> p (a e)")[:, 0:n],
+                in_=h_raw[:, a, c0 : c0 + n],
+                func=ACT.Copy,
+                accum_out=dv_s[:, a : a + 1],
+            )
+        for a, c0, n, slot in v_tasks:
+            junk_v = hg_pool.tile([P, 2, CH, 4], BF16, tag="hg", align_bytes=64)
+            half = n // 2
+            nc.vector.scalar_tensor_tensor(
+                out=junk_v[:].rearrange("p g e j -> p (g e j)")[:, 0:half],
+                in0=h_raw[:, a, c0 : c0 + half],
+                scalar=1.0,
+                in1=h_raw[:, a, c0 + half : c0 + n],
+                op0=ALU.mult,
+                op1=ALU.add,
+                accum_out=dv_v[:, a, slot : slot + 1],
+            )
+        dep = pb.tile([P, PLANES, E // P], F32, tag="b")
+        for a, c0, n in pieces:
+            for c in range(c0 // P, (c0 + n) // P):
+                nc.tensor.matmul(
+                    out=dep[:, a, c : c + 1],
+                    lhsT=h_raw[:, a, c * P : (c + 1) * P],
+                    rhs=ones[:, 0:1],
+                    start=True,
+                    stop=True,
+                )
+        deg = const.tile([P, PLANES + E // P], F32)
+        nc.vector.tensor_tensor(out=deg[:, 0:PLANES], in0=dv_v[:, :, 0], in1=dv_v[:, :, 1], op=ALU.add)
+        nc.vector.tensor_tensor(out=deg[:, 0:PLANES], in0=deg[:, 0:PLANES], in1=dv_s[:], op=ALU.add)
+        nc.vector.tensor_reduce(
+            out=deg[:, PLANES:], in_=dep[:].rearrange("p a c -> p c a"), axis=AX.X, op=ALU.add
+        )
+        nc.vector.tensor_scalar_max(out=deg[:], in0=deg[:], scalar1=1.0)
+        root = const.tile([P, PLANES + E // P], F32)
+        nc.scalar.activation(out=root[:], in_=deg[:], func=ACT.Sqrt)
+        rs = const.tile([P, PLANES + E // P], F32)
+        nc.vector.reciprocal(out=rs[:], in_=root[:])
+
+        re_b = const.tile([P, E], F32)
+        for r in range(ROUNDS):
+            spread = pa.tile([P, CH], F32, tag="a")
+            for q in range(SUB):
+                c = r * SUB + q
+                nc.tensor.transpose(
+                    out=spread[:, q * P : (q + 1) * P],
+                    in_=rs[:, PLANES + c : PLANES + c + 1].to_broadcast([P, P]),
+                    identity=ident[:],
+                )
+            if r % 2 == 0:
+                nc.scalar.copy(out=re_b[:, r * CH : (r + 1) * CH], in_=spread[:])
+            else:
+                nc.vector.tensor_copy(out=re_b[:, r * CH : (r + 1) * CH], in_=spread[:])
+
+        x0g = const.tile([P, 2, DIM, 4], BF16, align_bytes=64)
+        for g in range(2):
+            nc.vector.tensor_copy(
+                out=x0g[:, g].rearrange("p (t m) j -> p m j t", t=4),
+                in_=x0raw[:, g].rearrange("p j (m t) -> p m j t", t=4),
+            )
+        wg = const.tile([P, DIM, 4], BF16, align_bytes=64)
+        nc.vector.tensor_copy(
+            out=wg[:].rearrange("p (c i) t -> p c t i", i=4),
+            in_=wraw[:].rearrange("p t (c i) -> p c t i", i=4),
+        )
+        x0c = const.tile([P, 2, DIM], U32, align_bytes=64)
+        x0s = const.tile([P, 2, DIM], U8, align_bytes=64)
+        nc.vector.quantize_mx(
+            out=x0c[:].rearrange("p g c -> p (g c)").bitcast(FP8X4),
+            scales=x0s[:].rearrange("p g c -> p (g c)"),
+            in_=x0g[:].rearrange("p g c j -> p (g c j)"),
+        )
+        wc = const.tile([P, DIM], U32, align_bytes=64)
+        ws = const.tile([P, DIM], U8, align_bytes=64)
+        nc.vector.quantize_mx(
+            out=wc[:].bitcast(FP8X4), scales=ws[:], in_=wg[:].rearrange("p c t -> p (c t)")
+        )
+        gbr = const.tile([P, DIM], F32)
+        nc.vector.tensor_scalar_mul(out=gbr[:], in0=br_b[:], scalar1=g_col[:, 0:1])
+
+        x1_tiles = {}
+
+        def load_x1(r):
+            x1t = x1_pool.tile([P, SUB, DIM], BF16, tag="x1")
+            nc.sync.dma_start(
+                out=x1t[:],
+                in_=x_1_new[r * CH : (r + 1) * CH, :].rearrange("(s m) o -> m s o", m=P),
+            )
+            x1_tiles[r] = x1t
+
+        for r in range(3):
+            load_x1(r)
+
+        for r in range(ROUNDS):
+            cols = slice(r * CH, (r + 1) * CH)
+            tt = tt_pool.tile([P, PLANES, CH], BF16, tag="tt")
+            for a in range(PLANES):
+                nc.scalar.activation(
+                    out=tt[:, a, :], in_=re_b[:, cols], func=ACT.Copy, scale=rs[:, a : a + 1]
+                )
+            nc.vector.tensor_tensor(out=tt[:], in0=tt[:], in1=h_raw[:, :, cols], op=ALU.mult)
+            hg = hg_pool.tile([P, 2, CH, 4], BF16, tag="hg", align_bytes=64)
+            nc.vector.tensor_copy(
+                out=hg[:, 0].rearrange("p (c i) t -> p c t i", i=4),
+                in_=tt[:, 0:4, :].rearrange("p t (c i) -> p c t i", i=4),
+            )
+            nc.scalar.copy(
+                out=hg[:, 1].rearrange("p (c i) t -> p c t i", i=4),
+                in_=tt[:, 4:8, :].rearrange("p t (c i) -> p c t i", i=4),
+            )
+            hc = hq_pool.tile([P, 2, CH], U32, tag="hc", align_bytes=64)
+            hs = hq_pool.tile([P, 2, CH], U8, tag="hs", align_bytes=64)
+            nc.vector.quantize_mx(
+                out=hc[:].rearrange("p g c -> p (g c)").bitcast(FP8X4),
+                scales=hs[:].rearrange("p g c -> p (g c)"),
+                in_=hg[:].rearrange("p g c j -> p (g c j)"),
+            )
+            rg = rg_pool.tile([P, CH, 4], BF16, tag="rg", align_bytes=64)
+            for s in range(SUB):
+                e_sl = slice(s * P, (s + 1) * P)
+                ret = pa.tile([P, 4, P], F32, tag="a")
+                for t in range(4):
+                    d_sl = slice(t * P, (t + 1) * P)
+                    for g in range(2):
+                        nc.tensor.matmul_mx(
+                            out=ret[:, t, :],
+                            lhsT=x0c[:, g, d_sl].bitcast(FP8X4),
+                            lhsT_scale=x0s[:, g, d_sl],
+                            rhs=hc[:, g, e_sl].bitcast(FP8X4),
+                            rhs_scale=hs[:, g, e_sl],
+                            start=(g == 0),
+                            stop=(g == 1),
+                        )
+                nc.scalar.copy(out=rg[:, e_sl, :], in_=ret[:].rearrange("p t e -> p e t"))
+            rc = rg_pool.tile([P, CH], U32, tag="rc", align_bytes=64)
+            rsc = rg_pool.tile([P, CH], U8, tag="rsc", align_bytes=64)
+            nc.vector.quantize_mx(
+                out=rc[:].bitcast(FP8X4), scales=rsc[:], in_=rg[:].rearrange("p c t -> p (c t)")
+            )
+            ob = ob_pool.tile([P, SUB, DIM], F32, tag="ob")
+            nc.vector.tensor_tensor(
+                out=ob[:],
+                in0=x1_tiles[r][:],
+                in1=gbr[:].unsqueeze(1).to_broadcast([P, SUB, DIM]),
+                op=ALU.add,
+            )
+            if r + 3 < ROUNDS:
+                load_x1(r + 3)
+            for s in range(SUB):
+                e_sl = slice(s * P, (s + 1) * P)
+                upd = pb.tile([P, DIM], F32, tag="b")
+                nc.tensor.matmul_mx(
+                    out=upd[:],
+                    lhsT=rc[:, e_sl].bitcast(FP8X4),
+                    lhsT_scale=rsc[:, e_sl],
+                    rhs=wc[:].bitcast(FP8X4),
+                    rhs_scale=ws[:],
+                    start=True,
+                    stop=True,
+                )
+                nc.vector.scalar_tensor_tensor(
+                    out=ob[:, s, :],
+                    in0=upd[:],
+                    scalar=g_col[:, 0:1],
+                    in1=ob[:, s, :],
+                    op0=ALU.mult,
+                    op1=ALU.add,
+                )
+            nc.sync.dma_start(
+                out=out[r * CH : (r + 1) * CH, :].rearrange("(s m) o -> m s o", m=P), in_=ob[:]
+            )

@@ -23,6 +23,12 @@ CH = 512
 ROUNDS = E // CH
 SUB = CH // P
 
+T_ON_SCALAR = [3, 6, 3, 2, 1, 3, 2, 3]
+REGROUP = ["vv", "vs", "vv", "vv", "vv", "vv", "vv", "vv"]
+RET_OUT = ["ssss"] * 7 + ["vssv"]
+Y_OUT = ["ssss"] * 6 + ["svsv", "svsv"]
+Z_OUT = ["ssss", "ssss", "svss", "ssss", "ssss", "ssss", "sssv", "vvvs"]
+
 FLOPS = 2 * E * N_NODES * DIM + 2 * E * DIM * DIM
 
 
@@ -37,9 +43,11 @@ def tile_hypergraphgpslayer_pb_t_kernel(
         hq_pool = ctx.enter_context(tc.tile_pool(name="hq", bufs=2))
         rg_pool = ctx.enter_context(tc.tile_pool(name="rg", bufs=2))
         x1_pool = ctx.enter_context(tc.tile_pool(name="x1", bufs=3))
+        y_pool = ctx.enter_context(tc.tile_pool(name="y", bufs=2))
         ob_pool = ctx.enter_context(tc.tile_pool(name="ob", bufs=3))
-        pa = ctx.enter_context(tc.psum_pool(name="pa", bufs=4))
-        pb = ctx.enter_context(tc.psum_pool(name="pb", bufs=4))
+        pa = ctx.enter_context(tc.psum_pool(name="pa", bufs=3))
+        pb = ctx.enter_context(tc.psum_pool(name="pb", bufs=2))
+        pc = ctx.enter_context(tc.psum_pool(name="pc", bufs=3))
 
         gate_b = const.tile([P, 1], BF16)
         nc.sync.dma_start(out=gate_b[:], in_=gate_return.partition_broadcast(P))
@@ -59,11 +67,14 @@ def tile_hypergraphgpslayer_pb_t_kernel(
         )
         wraw = const.tile([P, 4, DIM], BF16)
         nc.sync.dma_start(out=wraw[:], in_=Wr.rearrange("(p t) o -> p t o", t=4))
-        br_b = const.tile([P, DIM], BF16)
-        nc.sync.dma_start(out=br_b[:], in_=br.partition_broadcast(P))
+        br_c = const.tile([P, 4], BF16)
+        with nc.allow_non_contiguous_dma(reason="512 bias values, one to a partition and column"):
+            nc.sync.dma_start(out=br_c[:], in_=br.rearrange("(q p) -> p q", p=P))
 
         ident = const.tile([P, P], F32)
         make_identity(nc, ident[:])
+        ident_bf = const.tile([P, P], BF16)
+        nc.vector.tensor_copy(out=ident_bf[:], in_=ident[:])
         ones = const.tile([P, 2], BF16)
         nc.vector.memset(ones[:], 1.0)
         dv_v = const.tile([P, PLANES, 2], F32)
@@ -166,8 +177,8 @@ def tile_hypergraphgpslayer_pb_t_kernel(
         nc.vector.quantize_mx(
             out=wc[:].bitcast(FP8X4), scales=ws[:], in_=wg[:].rearrange("p c t -> p (c t)")
         )
-        gbr = const.tile([P, DIM], F32)
-        nc.vector.tensor_scalar_mul(out=gbr[:], in0=br_b[:], scalar1=g_col[:, 0:1])
+        gbr = const.tile([P, 4], F32)
+        nc.vector.tensor_scalar_mul(out=gbr[:], in0=br_c[:], scalar1=g_col[:, 0:1])
 
         x1_tiles = {}
 
@@ -182,23 +193,42 @@ def tile_hypergraphgpslayer_pb_t_kernel(
         for r in range(3):
             load_x1(r)
 
-        for r in range(ROUNDS):
+        def leave_psum(engine, dst, src):
+            if engine == "s":
+                nc.scalar.copy(out=dst, in_=src)
+            else:
+                nc.vector.tensor_copy(out=dst, in_=src)
+
+        tt_tiles = {}
+
+        def make_t(r):
             cols = slice(r * CH, (r + 1) * CH)
             tt = tt_pool.tile([P, PLANES, CH], BF16, tag="tt")
             for a in range(PLANES):
-                nc.scalar.activation(
-                    out=tt[:, a, :], in_=re_b[:, cols], func=ACT.Copy, scale=rs[:, a : a + 1]
-                )
+                if a < T_ON_SCALAR[r]:
+                    nc.scalar.activation(
+                        out=tt[:, a, :], in_=re_b[:, cols], func=ACT.Copy, scale=rs[:, a : a + 1]
+                    )
+                else:
+                    nc.vector.tensor_scalar_mul(
+                        out=tt[:, a, :], in0=re_b[:, cols], scalar1=rs[:, a : a + 1]
+                    )
+            tt_tiles[r] = tt
+
+        make_t(0)
+        for r in range(ROUNDS):
+            cols = slice(r * CH, (r + 1) * CH)
+            if r + 1 < ROUNDS:
+                make_t(r + 1)
+            tt = tt_tiles[r]
             nc.vector.tensor_tensor(out=tt[:], in0=tt[:], in1=h_raw[:, :, cols], op=ALU.mult)
             hg = hg_pool.tile([P, 2, CH, 4], BF16, tag="hg", align_bytes=64)
-            nc.vector.tensor_copy(
-                out=hg[:, 0].rearrange("p (c i) t -> p c t i", i=4),
-                in_=tt[:, 0:4, :].rearrange("p t (c i) -> p c t i", i=4),
-            )
-            nc.scalar.copy(
-                out=hg[:, 1].rearrange("p (c i) t -> p c t i", i=4),
-                in_=tt[:, 4:8, :].rearrange("p t (c i) -> p c t i", i=4),
-            )
+            for g in range(2):
+                leave_psum(
+                    REGROUP[r][g],
+                    hg[:, g].rearrange("p (c i) t -> p c t i", i=4),
+                    tt[:, 4 * g : 4 * g + 4, :].rearrange("p t (c i) -> p c t i", i=4),
+                )
             hc = hq_pool.tile([P, 2, CH], U32, tag="hc", align_bytes=64)
             hs = hq_pool.tile([P, 2, CH], U8, tag="hs", align_bytes=64)
             nc.vector.quantize_mx(
@@ -222,41 +252,66 @@ def tile_hypergraphgpslayer_pb_t_kernel(
                             start=(g == 0),
                             stop=(g == 1),
                         )
-                nc.scalar.copy(out=rg[:, e_sl, :], in_=ret[:].rearrange("p t e -> p e t"))
+                leave_psum(RET_OUT[r][s], rg[:, e_sl, :], ret[:].rearrange("p t e -> p e t"))
             rc = rg_pool.tile([P, CH], U32, tag="rc", align_bytes=64)
             rsc = rg_pool.tile([P, CH], U8, tag="rsc", align_bytes=64)
             nc.vector.quantize_mx(
                 out=rc[:].bitcast(FP8X4), scales=rsc[:], in_=rg[:].rearrange("p c t -> p (c t)")
             )
-            ob = ob_pool.tile([P, SUB, DIM], F32, tag="ob")
-            nc.vector.tensor_tensor(
-                out=ob[:],
-                in0=x1_tiles[r][:],
-                in1=gbr[:].unsqueeze(1).to_broadcast([P, SUB, DIM]),
-                op=ALU.add,
-            )
-            if r + 3 < ROUNDS:
-                load_x1(r + 3)
-            for s in range(SUB):
-                e_sl = slice(s * P, (s + 1) * P)
-                upd = pb.tile([P, DIM], F32, tag="b")
+            y = y_pool.tile([P, 4, CH], F32, tag="y")
+            for q in range(4):
+                o_sl = slice(q * P, (q + 1) * P)
+                updT = pb.tile([P, CH], F32, tag="b")
                 nc.tensor.matmul_mx(
-                    out=upd[:],
-                    lhsT=rc[:, e_sl].bitcast(FP8X4),
-                    lhsT_scale=rsc[:, e_sl],
-                    rhs=wc[:].bitcast(FP8X4),
-                    rhs_scale=ws[:],
+                    out=updT[:],
+                    lhsT=wc[:, o_sl].bitcast(FP8X4),
+                    lhsT_scale=ws[:, o_sl],
+                    rhs=rc[:].bitcast(FP8X4),
+                    rhs_scale=rsc[:],
                     start=True,
                     stop=True,
                 )
-                nc.vector.scalar_tensor_tensor(
-                    out=ob[:, s, :],
-                    in0=upd[:],
-                    scalar=g_col[:, 0:1],
-                    in1=ob[:, s, :],
-                    op0=ALU.mult,
-                    op1=ALU.add,
-                )
+                if Y_OUT[r][q] == "s":
+                    nc.scalar.activation(
+                        out=y[:, q, :],
+                        in_=updT[:],
+                        func=ACT.Identity,
+                        bias=gbr[:, q : q + 1],
+                        scale=g_col[:, 0:1],
+                    )
+                else:
+                    nc.vector.tensor_scalar(
+                        out=y[:, q, :],
+                        in0=updT[:],
+                        scalar1=g_col[:, 0:1],
+                        scalar2=gbr[:, q : q + 1],
+                        op0=ALU.mult,
+                        op1=ALU.add,
+                    )
+            ob = ob_pool.tile([P, SUB, DIM], F32, tag="ob")
+            for s in range(SUB):
+                e_sl = slice(s * P, (s + 1) * P)
+                z = pc.tile([P, DIM], F32, tag="c")
+                for q in range(4):
+                    o_sl = slice(q * P, (q + 1) * P)
+                    nc.tensor.matmul(
+                        out=z[:, o_sl],
+                        lhsT=ident_bf[:],
+                        rhs=x1_tiles[r][:, s, o_sl],
+                        start=True,
+                        stop=False,
+                    )
+                    nc.tensor.matmul(
+                        out=z[:, o_sl],
+                        lhsT=y[:, q, e_sl],
+                        rhs=ident[:],
+                        is_transpose=True,
+                        start=False,
+                        stop=True,
+                    )
+                leave_psum(Z_OUT[r][s], ob[:, s, :], z[:])
+            if r + 3 < ROUNDS:
+                load_x1(r + 3)
             nc.sync.dma_start(
                 out=out[r * CH : (r + 1) * CH, :].rearrange("(s m) o -> m s o", m=P), in_=ob[:]
             )

@@ -23,11 +23,18 @@ CH = 512
 ROUNDS = E // CH
 SUB = CH // P
 
-T_ON_SCALAR = [3, 6, 3, 2, 1, 3, 2, 3]
-REGROUP = ["vv", "vs", "vv", "vv", "vv", "vv", "vv", "vv"]
-RET_OUT = ["ssss"] * 7 + ["vssv"]
-Y_OUT = ["ssss"] * 6 + ["svsv", "svsv"]
-Z_OUT = ["ssss", "ssss", "svss", "ssss", "ssss", "ssss", "sssv", "vvvs"]
+ROUND_PLAN = [
+    (512, 3, "ssss", "ssss", "ssss"),
+    (512, 4, "ssss", "ssss", "ssss"),
+    (512, 3, "ssss", "ssss", "ssss"),
+    (512, 2, "ssss", "ssss", "ssss"),
+    (512, 2, "ssss", "ssss", "ssss"),
+    (512, 2, "ssss", "ssss", "ssss"),
+    (512, 2, "ssss", "svsv", "svsv"),
+    (256, 2, "sv", "svsv", "sv"),
+    (128, 2, "s", "svsv", "s"),
+    (128, 2, "v", "svsv", "v"),
+]
 
 FLOPS = 2 * E * N_NODES * DIM + 2 * E * DIM * DIM
 
@@ -180,18 +187,21 @@ def tile_hypergraphgpslayer_pb_t_kernel(
         gbr = const.tile([P, 4], F32)
         nc.vector.tensor_scalar_mul(out=gbr[:], in0=br_c[:], scalar1=g_col[:, 0:1])
 
+        starts = [sum(plan[0] for plan in ROUND_PLAN[:k]) for k in range(len(ROUND_PLAN))]
+        n_rounds = len(ROUND_PLAN)
         x1_tiles = {}
 
-        def load_x1(r):
+        def load_x1(k):
+            n = ROUND_PLAN[k][0]
             x1t = x1_pool.tile([P, SUB, DIM], BF16, tag="x1")
             nc.sync.dma_start(
-                out=x1t[:],
-                in_=x_1_new[r * CH : (r + 1) * CH, :].rearrange("(s m) o -> m s o", m=P),
+                out=x1t[:, 0 : n // P, :],
+                in_=x_1_new[starts[k] : starts[k] + n, :].rearrange("(s m) o -> m s o", m=P),
             )
-            x1_tiles[r] = x1t
+            x1_tiles[k] = x1t
 
-        for r in range(3):
-            load_x1(r)
+        for k in range(3):
+            load_x1(k)
 
         def leave_psum(engine, dst, src):
             if engine == "s":
@@ -199,119 +209,110 @@ def tile_hypergraphgpslayer_pb_t_kernel(
             else:
                 nc.vector.tensor_copy(out=dst, in_=src)
 
-        tt_tiles = {}
-
-        def make_t(r):
-            cols = slice(r * CH, (r + 1) * CH)
+        for k in range(n_rounds):
+            n, t_on_s, ret_out, y_out, z_out = ROUND_PLAN[k]
+            cols = slice(starts[k], starts[k] + n)
             tt = tt_pool.tile([P, PLANES, CH], BF16, tag="tt")
             for a in range(PLANES):
-                if a < T_ON_SCALAR[r]:
+                if a < t_on_s:
                     nc.scalar.activation(
-                        out=tt[:, a, :], in_=re_b[:, cols], func=ACT.Copy, scale=rs[:, a : a + 1]
+                        out=tt[:, a, 0:n], in_=re_b[:, cols], func=ACT.Copy, scale=rs[:, a : a + 1]
                     )
                 else:
                     nc.vector.tensor_scalar_mul(
-                        out=tt[:, a, :], in0=re_b[:, cols], scalar1=rs[:, a : a + 1]
+                        out=tt[:, a, 0:n], in0=re_b[:, cols], scalar1=rs[:, a : a + 1]
                     )
-            tt_tiles[r] = tt
-
-        make_t(0)
-        for r in range(ROUNDS):
-            cols = slice(r * CH, (r + 1) * CH)
-            if r + 1 < ROUNDS:
-                make_t(r + 1)
-            tt = tt_tiles[r]
-            nc.vector.tensor_tensor(out=tt[:], in0=tt[:], in1=h_raw[:, :, cols], op=ALU.mult)
-            hg = hg_pool.tile([P, 2, CH, 4], BF16, tag="hg", align_bytes=64)
+            nc.vector.tensor_tensor(
+                out=tt[:, :, 0:n], in0=tt[:, :, 0:n], in1=h_raw[:, :, cols], op=ALU.mult
+            )
+            hg = hg_pool.tile([P, 2 * CH * 4], BF16, tag="hg", align_bytes=64)
+            hgv = hg[:, 0 : 8 * n].rearrange("p (g c j) -> p g c j", g=2, j=4)
             for g in range(2):
-                leave_psum(
-                    REGROUP[r][g],
-                    hg[:, g].rearrange("p (c i) t -> p c t i", i=4),
-                    tt[:, 4 * g : 4 * g + 4, :].rearrange("p t (c i) -> p c t i", i=4),
+                nc.vector.tensor_copy(
+                    out=hgv[:, g].rearrange("p (c i) t -> p c t i", i=4),
+                    in_=tt[:, 4 * g : 4 * g + 4, 0:n].rearrange("p t (c i) -> p c t i", i=4),
                 )
-            hc = hq_pool.tile([P, 2, CH], U32, tag="hc", align_bytes=64)
-            hs = hq_pool.tile([P, 2, CH], U8, tag="hs", align_bytes=64)
+            hc = hq_pool.tile([P, 2 * CH], U32, tag="hc", align_bytes=64)
+            hs = hq_pool.tile([P, 2 * CH], U8, tag="hs", align_bytes=64)
             nc.vector.quantize_mx(
-                out=hc[:].rearrange("p g c -> p (g c)").bitcast(FP8X4),
-                scales=hs[:].rearrange("p g c -> p (g c)"),
-                in_=hg[:].rearrange("p g c j -> p (g c j)"),
+                out=hc[:, 0 : 2 * n].bitcast(FP8X4), scales=hs[:, 0 : 2 * n], in_=hg[:, 0 : 8 * n]
             )
             rg = rg_pool.tile([P, CH, 4], BF16, tag="rg", align_bytes=64)
-            for s in range(SUB):
+            for s in range(n // P):
                 e_sl = slice(s * P, (s + 1) * P)
                 ret = pa.tile([P, 4, P], F32, tag="a")
                 for t in range(4):
                     d_sl = slice(t * P, (t + 1) * P)
                     for g in range(2):
+                        h_sl = slice(g * n + s * P, g * n + (s + 1) * P)
                         nc.tensor.matmul_mx(
                             out=ret[:, t, :],
                             lhsT=x0c[:, g, d_sl].bitcast(FP8X4),
                             lhsT_scale=x0s[:, g, d_sl],
-                            rhs=hc[:, g, e_sl].bitcast(FP8X4),
-                            rhs_scale=hs[:, g, e_sl],
+                            rhs=hc[:, h_sl].bitcast(FP8X4),
+                            rhs_scale=hs[:, h_sl],
                             start=(g == 0),
                             stop=(g == 1),
                         )
-                leave_psum(RET_OUT[r][s], rg[:, e_sl, :], ret[:].rearrange("p t e -> p e t"))
+                leave_psum(ret_out[s], rg[:, e_sl, :], ret[:].rearrange("p t e -> p e t"))
             rc = rg_pool.tile([P, CH], U32, tag="rc", align_bytes=64)
             rsc = rg_pool.tile([P, CH], U8, tag="rsc", align_bytes=64)
             nc.vector.quantize_mx(
-                out=rc[:].bitcast(FP8X4), scales=rsc[:], in_=rg[:].rearrange("p c t -> p (c t)")
+                out=rc[:, 0:n].bitcast(FP8X4),
+                scales=rsc[:, 0:n],
+                in_=rg[:, 0:n, :].rearrange("p c t -> p (c t)"),
             )
             y = y_pool.tile([P, 4, CH], F32, tag="y")
             for q in range(4):
                 o_sl = slice(q * P, (q + 1) * P)
                 updT = pb.tile([P, CH], F32, tag="b")
                 nc.tensor.matmul_mx(
-                    out=updT[:],
+                    out=updT[:, 0:n],
                     lhsT=wc[:, o_sl].bitcast(FP8X4),
                     lhsT_scale=ws[:, o_sl],
-                    rhs=rc[:].bitcast(FP8X4),
-                    rhs_scale=rsc[:],
+                    rhs=rc[:, 0:n].bitcast(FP8X4),
+                    rhs_scale=rsc[:, 0:n],
                     start=True,
                     stop=True,
                 )
-                if Y_OUT[r][q] == "s":
+                if y_out[q] == "s":
                     nc.scalar.activation(
-                        out=y[:, q, :],
-                        in_=updT[:],
+                        out=y[:, q, 0:n],
+                        in_=updT[:, 0:n],
                         func=ACT.Identity,
                         bias=gbr[:, q : q + 1],
                         scale=g_col[:, 0:1],
                     )
                 else:
                     nc.vector.tensor_scalar(
-                        out=y[:, q, :],
-                        in0=updT[:],
+                        out=y[:, q, 0:n],
+                        in0=updT[:, 0:n],
                         scalar1=g_col[:, 0:1],
                         scalar2=gbr[:, q : q + 1],
                         op0=ALU.mult,
                         op1=ALU.add,
                     )
             ob = ob_pool.tile([P, SUB, DIM], F32, tag="ob")
-            for s in range(SUB):
+            for s in range(n // P):
                 e_sl = slice(s * P, (s + 1) * P)
                 z = pc.tile([P, DIM], F32, tag="c")
+                nc.tensor.matmul(
+                    out=z[:], lhsT=ident_bf[:], rhs=x1_tiles[k][:, s, :], start=True, stop=False
+                )
                 for q in range(4):
                     o_sl = slice(q * P, (q + 1) * P)
-                    nc.tensor.matmul(
-                        out=z[:, o_sl],
-                        lhsT=ident_bf[:],
-                        rhs=x1_tiles[r][:, s, o_sl],
-                        start=True,
-                        stop=False,
-                    )
                     nc.tensor.matmul(
                         out=z[:, o_sl],
                         lhsT=y[:, q, e_sl],
                         rhs=ident[:],
                         is_transpose=True,
                         start=False,
-                        stop=True,
+                        stop=(q == 3),
                     )
-                leave_psum(Z_OUT[r][s], ob[:, s, :], z[:])
-            if r + 3 < ROUNDS:
-                load_x1(r + 3)
+                leave_psum(z_out[s], ob[:, s, :], z[:])
+            if k + 3 < n_rounds:
+                load_x1(k + 3)
             nc.sync.dma_start(
-                out=out[r * CH : (r + 1) * CH, :].rearrange("(s m) o -> m s o", m=P), in_=ob[:]
+                out=out[starts[k] : starts[k] + n, :].rearrange("(s m) o -> m s o", m=P),
+                in_=ob[:, 0 : n // P, :],
             )

@@ -23,17 +23,25 @@ CH = 512
 ROUNDS = E // CH
 SUB = CH // P
 
+T_PLAN = [(256, 3), (256, 3), (512, 4), (512, 3), (512, 2), (512, 2), (512, 2), (512, 2), (512, 2)]
 ROUND_PLAN = [
-    (512, 3, "ssss", "ssss", "ssss"),
-    (512, 4, "ssss", "ssss", "ssss"),
-    (512, 3, "ssss", "ssss", "ssss"),
-    (512, 2, "ssss", "ssss", "ssss"),
-    (512, 2, "ssss", "ssss", "ssss"),
-    (512, 2, "ssss", "ssss", "ssss"),
-    (512, 2, "ssss", "svsv", "svsv"),
-    (256, 2, "sv", "svsv", "sv"),
-    (128, 2, "s", "svsv", "s"),
-    (128, 2, "v", "svsv", "v"),
+    (256, 3, "ss", "ssss", "ss", "vv"),
+    (256, 3, "ss", "ssss", "ss", "vv"),
+    (256, 4, "ss", "ssss", "ss", "vs"),
+    (256, 4, "ss", "ssss", "ss", "vs"),
+    (256, 3, "ss", "ssss", "ss", "vv"),
+    (256, 3, "ss", "ssss", "ss", "vv"),
+    (256, 2, "ss", "ssss", "ss", "vv"),
+    (256, 2, "ss", "ssss", "ss", "vv"),
+    (256, 2, "ss", "ssss", "ss", "vv"),
+    (256, 2, "ss", "ssss", "ss", "vv"),
+    (256, 2, "ss", "ssss", "ss", "vv"),
+    (256, 2, "ss", "ssss", "ss", "vv"),
+    (256, 2, "ss", "svsv", "ss", "vv"),
+    (256, 2, "ss", "svsv", "sv", "vv"),
+    (256, 3, "sv", "sssv", "sv", "vv"),
+    (128, 2, "s", "ssvv", "s", "vv"),
+    (128, 1, "v", "svsv", "v", "vv"),
 ]
 
 FLOPS = 2 * E * N_NODES * DIM + 2 * E * DIM * DIM
@@ -156,10 +164,10 @@ def tile_hypergraphgpslayer_pb_t_kernel(
                     in_=rs[:, PLANES + c : PLANES + c + 1].to_broadcast([P, P]),
                     identity=ident[:],
                 )
-            if r % 2 == 0:
-                nc.scalar.copy(out=re_b[:, r * CH : (r + 1) * CH], in_=spread[:])
-            else:
+            if r in (1, 3):
                 nc.vector.tensor_copy(out=re_b[:, r * CH : (r + 1) * CH], in_=spread[:])
+            else:
+                nc.scalar.copy(out=re_b[:, r * CH : (r + 1) * CH], in_=spread[:])
 
         x0g = const.tile([P, 2, DIM, 4], BF16, align_bytes=64)
         for g in range(2):
@@ -209,28 +217,45 @@ def tile_hypergraphgpslayer_pb_t_kernel(
             else:
                 nc.vector.tensor_copy(out=dst, in_=src)
 
-        for k in range(n_rounds):
-            n, t_on_s, ret_out, y_out, z_out = ROUND_PLAN[k]
-            cols = slice(starts[k], starts[k] + n)
+        t_starts = [sum(plan[0] for plan in T_PLAN[:b]) for b in range(len(T_PLAN))]
+        t_now = [None, 0]
+
+        def make_t(b):
+            width, t_on_s = T_PLAN[b]
+            t_cols = slice(t_starts[b], t_starts[b] + width)
             tt = tt_pool.tile([P, PLANES, CH], BF16, tag="tt")
             for a in range(PLANES):
                 if a < t_on_s:
                     nc.scalar.activation(
-                        out=tt[:, a, 0:n], in_=re_b[:, cols], func=ACT.Copy, scale=rs[:, a : a + 1]
+                        out=tt[:, a, 0:width],
+                        in_=re_b[:, t_cols],
+                        func=ACT.Copy,
+                        scale=rs[:, a : a + 1],
                     )
                 else:
                     nc.vector.tensor_scalar_mul(
-                        out=tt[:, a, 0:n], in0=re_b[:, cols], scalar1=rs[:, a : a + 1]
+                        out=tt[:, a, 0:width], in0=re_b[:, t_cols], scalar1=rs[:, a : a + 1]
                     )
+            t_now[0] = tt
+            t_now[1] = t_starts[b]
+
+        for k in range(n_rounds):
+            n, t_on_s, ret_out, y_out, z_out, regroup_on = ROUND_PLAN[k]
+            cols = slice(starts[k], starts[k] + n)
+            if starts[k] in t_starts:
+                make_t(t_starts.index(starts[k]))
+            tt, t_first = t_now[0], t_now[1]
+            mine = slice(starts[k] - t_first, starts[k] - t_first + n)
             nc.vector.tensor_tensor(
-                out=tt[:, :, 0:n], in0=tt[:, :, 0:n], in1=h_raw[:, :, cols], op=ALU.mult
+                out=tt[:, :, mine], in0=tt[:, :, mine], in1=h_raw[:, :, cols], op=ALU.mult
             )
             hg = hg_pool.tile([P, 2 * CH * 4], BF16, tag="hg", align_bytes=64)
             hgv = hg[:, 0 : 8 * n].rearrange("p (g c j) -> p g c j", g=2, j=4)
             for g in range(2):
-                nc.vector.tensor_copy(
-                    out=hgv[:, g].rearrange("p (c i) t -> p c t i", i=4),
-                    in_=tt[:, 4 * g : 4 * g + 4, 0:n].rearrange("p t (c i) -> p c t i", i=4),
+                leave_psum(
+                    regroup_on[g],
+                    hgv[:, g].rearrange("p (c i) t -> p c t i", i=4),
+                    tt[:, 4 * g : 4 * g + 4, mine].rearrange("p t (c i) -> p c t i", i=4),
                 )
             hc = hq_pool.tile([P, 2 * CH], U32, tag="hc", align_bytes=64)
             hs = hq_pool.tile([P, 2 * CH], U8, tag="hs", align_bytes=64)

@@ -20,28 +20,23 @@ E = 4096
 DIM = 512
 PLANES = 8
 CH = 512
-ROUNDS = E // CH
 SUB = CH // P
+TINY = 1e-20
+CUT7 = 2560
+BLOCKS = [(0, 512), (512, 512), (1024, 1024), (2048, 1024), (3072, 1024)]
 
-T_PLAN = [(256, 3), (256, 3), (512, 4), (512, 3), (512, 2), (512, 2), (512, 2), (512, 2), (512, 2)]
 ROUND_PLAN = [
-    (256, 3, "ss", "ssss", "ss", "vv"),
-    (256, 3, "ss", "ssss", "ss", "vv"),
-    (256, 4, "ss", "ssss", "ss", "vs"),
-    (256, 4, "ss", "ssss", "ss", "vs"),
-    (256, 3, "ss", "ssss", "ss", "vv"),
-    (256, 3, "ss", "ssss", "ss", "vv"),
-    (256, 2, "ss", "ssss", "ss", "vv"),
-    (256, 2, "ss", "ssss", "ss", "vv"),
-    (256, 2, "ss", "ssss", "ss", "vv"),
-    (256, 2, "ss", "ssss", "ss", "vv"),
-    (256, 2, "ss", "ssss", "ss", "vv"),
-    (256, 2, "ss", "ssss", "ss", "vv"),
-    (256, 2, "ss", "svsv", "ss", "vv"),
-    (256, 2, "ss", "svsv", "sv", "vv"),
-    (256, 3, "sv", "sssv", "sv", "vv"),
-    (128, 2, "s", "ssvv", "s", "vv"),
-    (128, 1, "v", "svsv", "v", "vv"),
+    (256, "ss", "ssss", "ss"),
+    (256, "ss", "ssss", "ss"),
+    (512, "ssss", "ssss", "ssss"),
+    (512, "ssss", "ssss", "ssss"),
+    (512, "ssss", "ssss", "ssss"),
+    (512, "ssss", "ssss", "ssss"),
+    (512, "ssss", "ssss", "ssss"),
+    (512, "ssss", "ssss", "ssss"),
+    (256, "ss", "ssss", "sv"),
+    (128, "s", "ssvv", "s"),
+    (128, "v", "svsv", "v"),
 ]
 
 FLOPS = 2 * E * N_NODES * DIM + 2 * E * DIM * DIM
@@ -53,38 +48,41 @@ def tile_hypergraphgpslayer_pb_t_kernel(
     nc = tc.nc
     with ExitStack() as ctx:
         const = ctx.enter_context(tc.tile_pool(name="const", bufs=1))
-        tt_pool = ctx.enter_context(tc.tile_pool(name="tt", bufs=3))
-        hg_pool = ctx.enter_context(tc.tile_pool(name="hg", bufs=2))
+        ha = ctx.enter_context(tc.tile_pool(name="ha", bufs=4))
+        hb = ctx.enter_context(tc.tile_pool(name="hb", bufs=4))
         hq_pool = ctx.enter_context(tc.tile_pool(name="hq", bufs=2))
         rg_pool = ctx.enter_context(tc.tile_pool(name="rg", bufs=2))
         x1_pool = ctx.enter_context(tc.tile_pool(name="x1", bufs=3))
-        y_pool = ctx.enter_context(tc.tile_pool(name="y", bufs=2))
-        ob_pool = ctx.enter_context(tc.tile_pool(name="ob", bufs=3))
-        pa = ctx.enter_context(tc.psum_pool(name="pa", bufs=3))
+        ps = ctx.enter_context(tc.psum_pool(name="ps", bufs=2))
+        pa = ctx.enter_context(tc.psum_pool(name="pa", bufs=2))
         pb = ctx.enter_context(tc.psum_pool(name="pb", bufs=2))
-        pc = ctx.enter_context(tc.psum_pool(name="pc", bufs=3))
+        pc = ctx.enter_context(tc.psum_pool(name="pc", bufs=2))
 
         gate_b = const.tile([P, 1], BF16)
-        nc.sync.dma_start(out=gate_b[:], in_=gate_return.partition_broadcast(P))
+        nc.scalar.dma_start(out=gate_b[:], in_=gate_return.partition_broadcast(P))
+        br_c = const.tile([P, 4], BF16)
+        with nc.allow_non_contiguous_dma(reason="512 bias values, one to a partition and column"):
+            nc.scalar.dma_start(out=br_c[:], in_=br.rearrange("(q p) -> p q", p=P))
 
-        h_raw = const.tile([P, PLANES, E], BF16)
         h_dram = incidence_1.rearrange("(g p j) e -> p g j e", g=2, j=4)
-        pieces = [(a, 0, E) for a in range(PLANES - 1)] + [
-            (PLANES - 1, 0, E // 2),
-            (PLANES - 1, E // 2, E // 2),
-        ]
-        for a, c0, n in pieces:
-            nc.sync.dma_start(out=h_raw[:, a, c0 : c0 + n], in_=h_dram[:, a // 4, a % 4, c0 : c0 + n])
+        h_raw = []
+        pieces = []
+        for a in range(PLANES):
+            pool = ha if a < 4 else hb
+            h_a = pool.tile([P, E], BF16, tag="big", align_bytes=64, name="h_a")
+            cuts = [(0, E)] if a < PLANES - 1 else [(0, CUT7), (CUT7, E - CUT7)]
+            for c0, n in cuts:
+                nc.sync.dma_start(out=h_a[:, c0 : c0 + n], in_=h_dram[:, a // 4, a % 4, c0 : c0 + n])
+                pieces.append((a, c0, n))
+            h_raw.append(h_a)
 
-        x0raw = const.tile([P, 2, 4, DIM], BF16)
+        x0raw = ha.tile([P, 2, 4, DIM], BF16, tag="big", align_bytes=64)
         nc.sync.dma_start(
             out=x0raw[:], in_=x_0_local.rearrange("(g p j) d -> p g j d", g=2, j=4)
         )
-        wraw = const.tile([P, 4, DIM], BF16)
-        nc.sync.dma_start(out=wraw[:], in_=Wr.rearrange("(p t) o -> p t o", t=4))
-        br_c = const.tile([P, 4], BF16)
-        with nc.allow_non_contiguous_dma(reason="512 bias values, one to a partition and column"):
-            nc.sync.dma_start(out=br_c[:], in_=br.rearrange("(q p) -> p q", p=P))
+        wst = ha.tile([P, 2, 4 * DIM], BF16, tag="big", align_bytes=64)
+        wraw = wst[:, 0].rearrange("p (t o) -> p t o", t=4)
+        nc.sync.dma_start(out=wraw, in_=Wr.rearrange("(p t) o -> p t o", t=4))
 
         ident = const.tile([P, P], F32)
         make_identity(nc, ident[:])
@@ -92,112 +90,153 @@ def tile_hypergraphgpslayer_pb_t_kernel(
         nc.vector.tensor_copy(out=ident_bf[:], in_=ident[:])
         ones = const.tile([P, 2], BF16)
         nc.vector.memset(ones[:], 1.0)
-        dv_v = const.tile([P, PLANES, 2], F32)
-        nc.vector.memset(dv_v[:], 0.0)
-        dv_s = const.tile([P, PLANES], F32)
-        nc.vector.memset(dv_s[:], 0.0)
+        tiny = const.tile([P, 1], F32)
+        nc.vector.memset(tiny[:], TINY)
 
         g_col = const.tile([P, 1], F32)
         nc.scalar.activation(out=g_col[:], in_=gate_b[:], func=ACT.Tanh)
         warm = const.tile([P, 1], F32)
-        nc.scalar.activation(out=warm[:], in_=g_col[:], func=ACT.Sqrt, bias=1.0, scale=0.0)
+        nc.scalar.activation(
+            out=warm[:], in_=g_col[:], func=ACT.Abs_reciprocal_sqrt, bias=1.0, scale=0.0
+        )
+        gbr = const.tile([P, 4], F32)
+        nc.scalar.activation(out=gbr[:], in_=br_c[:], func=ACT.Copy, scale=g_col[:, 0:1])
 
-        s_tasks = [(0, 0, 4096), (2, 0, 4096), (4, 0, 2048), (6, 2048, 2048), (7, 3072, 1024)]
-        v_tasks = [
-            (1, 0, 4096, 0),
-            (3, 0, 4096, 0),
-            (4, 2048, 2048, 0),
-            (5, 0, 4096, 0),
-            (6, 0, 2048, 0),
-            (7, 0, 2048, 0),
-            (7, 2048, 1024, 1),
-        ]
-        for a, c0, n in s_tasks:
-            junk_s = tt_pool.tile([P, PLANES, CH], BF16, tag="tt")
-            nc.scalar.activation(
-                out=junk_s[:].rearrange("p a e -> p (a e)")[:, 0:n],
-                in_=h_raw[:, a, c0 : c0 + n],
-                func=ACT.Copy,
-                accum_out=dv_s[:, a : a + 1],
+        ctx.enter_context(
+            tc.manual_schedule(
+                engines={mybir.EngineType.DVE, mybir.EngineType.Activation, mybir.EngineType.PE}
             )
-        for a, c0, n, slot in v_tasks:
-            junk_v = hg_pool.tile([P, 2, CH, 4], BF16, tag="hg", align_bytes=64)
-            half = n // 2
-            nc.vector.scalar_tensor_tensor(
-                out=junk_v[:].rearrange("p g e j -> p (g e j)")[:, 0:half],
-                in0=h_raw[:, a, c0 : c0 + half],
-                scalar=1.0,
-                in1=h_raw[:, a, c0 + half : c0 + n],
+        )
+
+        dv = const.tile([P, PLANES + 1], F32)
+        rv = const.tile([P, PLANES], F32)
+        hr = [
+            const.tile([P, PLANES, n], F32, name="hr%d" % b) for b, (c0, n) in enumerate(BLOCKS)
+        ]
+
+        def block_of(c0):
+            return max(b for b in range(len(BLOCKS)) if BLOCKS[b][0] <= c0)
+
+        dep = pc.tile([P, PLANES, E // P], F32, tag="c")
+
+        def unread(a):
+            two = a - a % 2
+            return hr[a % 2 - 2][:, two : two + 2, :].rearrange("p a e -> p (a e)").bitcast(BF16)
+
+        def row_sums(a, c0, n, slot, first):
+            nc.vector.tensor_scalar(
+                out=unread(a)[:, c0 : c0 + n],
+                in0=h_raw[a][:, c0 : c0 + n],
+                scalar1=1.0,
+                scalar2=first,
                 op0=ALU.mult,
                 op1=ALU.add,
-                accum_out=dv_v[:, a, slot : slot + 1],
+                accum_out=dv[:, slot : slot + 1],
             )
-        dep = pb.tile([P, PLANES, E // P], F32, tag="b")
+
+        def inverse_root(a, bias=0.0):
+            nc.scalar.activation(
+                out=rv[:, a : a + 1], in_=dv[:, a : a + 1], func=ACT.Abs_reciprocal_sqrt, bias=bias
+            )
+
+        def scale_rows(engine, a, c0, c1):
+            while c0 < c1:
+                b = block_of(c0)
+                first = BLOCKS[b][0]
+                c = min(c1, first + BLOCKS[b][1])
+                dst = hr[b][:, a, c0 - first : c - first]
+                src, by = h_raw[a][:, c0:c], rv[:, a : a + 1]
+                if engine == "s":
+                    nc.scalar.activation(out=dst, in_=src, func=ACT.Copy, scale=by)
+                else:
+                    nc.gpsimd.tensor_scalar(
+                        out=dst, in0=src, scalar1=by, scalar2=0.0, op0=ALU.mult, op1=ALU.add
+                    )
+                c0 = c
+
         for a, c0, n in pieces:
             for c in range(c0 // P, (c0 + n) // P):
                 nc.tensor.matmul(
                     out=dep[:, a, c : c + 1],
-                    lhsT=h_raw[:, a, c * P : (c + 1) * P],
+                    lhsT=h_raw[a][:, c * P : (c + 1) * P],
                     rhs=ones[:, 0:1],
                     start=True,
                     stop=True,
                 )
-        deg = const.tile([P, PLANES + E // P], F32)
-        nc.vector.tensor_tensor(out=deg[:, 0:PLANES], in0=dv_v[:, :, 0], in1=dv_v[:, :, 1], op=ALU.add)
-        nc.vector.tensor_tensor(out=deg[:, 0:PLANES], in0=deg[:, 0:PLANES], in1=dv_s[:], op=ALU.add)
+
+        for a in range(PLANES - 1):
+            row_sums(a, 0, E, a, TINY)
+        row_sums(7, 0, CUT7, 7, TINY)
+        de = const.tile([P, E // P], F32)
         nc.vector.tensor_reduce(
-            out=deg[:, PLANES:], in_=dep[:].rearrange("p a c -> p c a"), axis=AX.X, op=ALU.add
+            out=de[:], in_=dep[:].rearrange("p a c -> p c a"), axis=AX.X, op=ALU.add
         )
-        nc.vector.tensor_scalar_max(out=deg[:], in0=deg[:], scalar1=1.0)
-        root = const.tile([P, PLANES + E // P], F32)
-        nc.scalar.activation(out=root[:], in_=deg[:], func=ACT.Sqrt)
-        rs = const.tile([P, PLANES + E // P], F32)
-        nc.vector.reciprocal(out=rs[:], in_=root[:])
+        rs = const.tile([P, E // P], F32)
 
-        re_b = const.tile([P, E], F32)
-        for r in range(ROUNDS):
-            spread = pa.tile([P, CH], F32, tag="a")
-            for q in range(SUB):
-                c = r * SUB + q
-                nc.tensor.transpose(
-                    out=spread[:, q * P : (q + 1) * P],
-                    in_=rs[:, PLANES + c : PLANES + c + 1].to_broadcast([P, P]),
-                    identity=ident[:],
-                )
-            if r in (1, 3):
-                nc.vector.tensor_copy(out=re_b[:, r * CH : (r + 1) * CH], in_=spread[:])
-            else:
-                nc.scalar.copy(out=re_b[:, r * CH : (r + 1) * CH], in_=spread[:])
+        for a in (0, 2):
+            inverse_root(a)
+            scale_rows("s", a, 0, E // 2)
+            inverse_root(a + 1)
+            scale_rows("s", a, E // 2, E)
+        inverse_root(4)
+        scale_rows("s", 4, 0, E // 2)
+        inverse_root(5)
+        scale_rows("s", 4, E // 2, 3 * E // 4)
+        nc.scalar.activation(
+            out=unread(7)[:, CUT7:],
+            in_=h_raw[7][:, CUT7:],
+            func=ACT.Copy,
+            accum_out=dv[:, 8:9],
+        )
+        inverse_root(6)
+        nc.scalar.activation(
+            out=rs[:], in_=de[:], func=ACT.Abs_reciprocal_sqrt, bias=tiny[:, 0:1]
+        )
+        inverse_root(7, dv[:, 8:9])
+        scale_rows("s", 6, 0, CH)
+        scale_rows("s", 7, 0, CH)
+        for a in (1, 3, 5):
+            scale_rows("g", a, 0, E)
 
-        x0g = const.tile([P, 2, DIM, 4], BF16, align_bytes=64)
+        def scale_the_rest():
+            scale_rows("s", 6, CH, 1024)
+            scale_rows("s", 4, 3 * E // 4, E)
+            scale_rows("s", 6, 1024, E // 2)
+            for c in range(CH, E, CH):
+                scale_rows("g", 7, c, c + CH)
+                if c >= E // 2:
+                    scale_rows("g", 6, c, c + CH)
+
+        x0g = ha.tile([P, 2, DIM, 4], BF16, tag="big", align_bytes=64)
         for g in range(2):
             nc.vector.tensor_copy(
                 out=x0g[:, g].rearrange("p (t m) j -> p m j t", t=4),
                 in_=x0raw[:, g].rearrange("p j (m t) -> p m j t", t=4),
             )
-        wg = const.tile([P, DIM, 4], BF16, align_bytes=64)
-        nc.vector.tensor_copy(
-            out=wg[:].rearrange("p (c i) t -> p c t i", i=4),
-            in_=wraw[:].rearrange("p t (c i) -> p c t i", i=4),
-        )
         x0c = const.tile([P, 2, DIM], U32, align_bytes=64)
         x0s = const.tile([P, 2, DIM], U8, align_bytes=64)
-        nc.vector.quantize_mx(
-            out=x0c[:].rearrange("p g c -> p (g c)").bitcast(FP8X4),
-            scales=x0s[:].rearrange("p g c -> p (g c)"),
-            in_=x0g[:].rearrange("p g c j -> p (g c j)"),
-        )
         wc = const.tile([P, DIM], U32, align_bytes=64)
         ws = const.tile([P, DIM], U8, align_bytes=64)
-        nc.vector.quantize_mx(
-            out=wc[:].bitcast(FP8X4), scales=ws[:], in_=wg[:].rearrange("p c t -> p (c t)")
-        )
-        gbr = const.tile([P, 4], F32)
-        nc.vector.tensor_scalar_mul(out=gbr[:], in0=br_c[:], scalar1=g_col[:, 0:1])
+
+        def quantise_x0():
+            nc.vector.quantize_mx(
+                out=x0c[:].rearrange("p g c -> p (g c)").bitcast(FP8X4),
+                scales=x0s[:].rearrange("p g c -> p (g c)"),
+                in_=x0g[:].rearrange("p g c j -> p (g c j)"),
+            )
+
+        def regroup_w():
+            nc.vector.tensor_copy(
+                out=wst[:, 1].rearrange("p (c i t) -> p c t i", i=4, t=4),
+                in_=wst[:, 0].rearrange("p (t c i) -> p c t i", i=4, t=4),
+            )
+
+        def quantise_w():
+            nc.vector.quantize_mx(out=wc[:].bitcast(FP8X4), scales=ws[:], in_=wst[:, 1])
 
         starts = [sum(plan[0] for plan in ROUND_PLAN[:k]) for k in range(len(ROUND_PLAN))]
         n_rounds = len(ROUND_PLAN)
-        x1_tiles = {}
+        x1_tiles, spreads, groups, codes, rets, ret_codes = {}, {}, {}, {}, {}, {}
 
         def load_x1(k):
             n = ROUND_PLAN[k][0]
@@ -208,63 +247,68 @@ def tile_hypergraphgpslayer_pb_t_kernel(
             )
             x1_tiles[k] = x1t
 
-        for k in range(3):
-            load_x1(k)
-
         def leave_psum(engine, dst, src):
             if engine == "s":
                 nc.scalar.copy(out=dst, in_=src)
             else:
                 nc.vector.tensor_copy(out=dst, in_=src)
 
-        t_starts = [sum(plan[0] for plan in T_PLAN[:b]) for b in range(len(T_PLAN))]
-        t_now = [None, 0]
-
-        def make_t(b):
-            width, t_on_s = T_PLAN[b]
-            t_cols = slice(t_starts[b], t_starts[b] + width)
-            tt = tt_pool.tile([P, PLANES, CH], BF16, tag="tt")
-            for a in range(PLANES):
-                if a < t_on_s:
-                    nc.scalar.activation(
-                        out=tt[:, a, 0:width],
-                        in_=re_b[:, t_cols],
-                        func=ACT.Copy,
-                        scale=rs[:, a : a + 1],
-                    )
-                else:
-                    nc.vector.tensor_scalar_mul(
-                        out=tt[:, a, 0:width], in0=re_b[:, t_cols], scalar1=rs[:, a : a + 1]
-                    )
-            t_now[0] = tt
-            t_now[1] = t_starts[b]
-
-        for k in range(n_rounds):
-            n, t_on_s, ret_out, y_out, z_out, regroup_on = ROUND_PLAN[k]
-            cols = slice(starts[k], starts[k] + n)
-            if starts[k] in t_starts:
-                make_t(t_starts.index(starts[k]))
-            tt, t_first = t_now[0], t_now[1]
-            mine = slice(starts[k] - t_first, starts[k] - t_first + n)
-            nc.vector.tensor_tensor(
-                out=tt[:, :, mine], in0=tt[:, :, mine], in1=h_raw[:, :, cols], op=ALU.mult
-            )
-            hg = hg_pool.tile([P, 2 * CH * 4], BF16, tag="hg", align_bytes=64)
-            hgv = hg[:, 0 : 8 * n].rearrange("p (g c j) -> p g c j", g=2, j=4)
-            for g in range(2):
-                leave_psum(
-                    regroup_on[g],
-                    hgv[:, g].rearrange("p (c i) t -> p c t i", i=4),
-                    tt[:, 4 * g : 4 * g + 4, mine].rearrange("p t (c i) -> p c t i", i=4),
+        def spread(k):
+            n = ROUND_PLAN[k][0]
+            sp = ps.tile([P, CH], F32, tag="s")
+            for q in range(n // P):
+                c = starts[k] // P + q
+                nc.tensor.transpose(
+                    out=sp[:, q * P : (q + 1) * P],
+                    in_=rs[:, c : c + 1].to_broadcast([P, P]),
+                    identity=ident[:],
                 )
+            spreads[k] = sp
+
+        def normalise(k):
+            n = ROUND_PLAN[k][0]
+            b = block_of(starts[k])
+            c0 = starts[k] - BLOCKS[b][0]
+            hg = ha.tile([P, 2 * CH * 4], BF16, tag="big", align_bytes=64)
+            hgv = hg[:, 0 : 8 * n].rearrange("p (g c i t) -> p g c t i", g=2, i=2, t=4)
+            by = (
+                spreads[k][:, 0:n]
+                .rearrange("p (c i) -> p c i", i=2)
+                .unsqueeze(2)
+                .to_broadcast([P, n // 2, 4, 2])
+            )
+            for g in range(2):
+                nc.vector.tensor_tensor(
+                    out=hgv[:, g],
+                    in0=hr[b][:, 4 * g : 4 * g + 4, c0 : c0 + n].rearrange(
+                        "p t (c i) -> p c t i", i=2
+                    ),
+                    in1=by,
+                    op=ALU.mult,
+                )
+            groups[k] = hg
+
+        def quantise_h(k):
+            n = ROUND_PLAN[k][0]
             hc = hq_pool.tile([P, 2 * CH], U32, tag="hc", align_bytes=64)
             hs = hq_pool.tile([P, 2 * CH], U8, tag="hs", align_bytes=64)
             nc.vector.quantize_mx(
-                out=hc[:, 0 : 2 * n].bitcast(FP8X4), scales=hs[:, 0 : 2 * n], in_=hg[:, 0 : 8 * n]
+                out=hc[:, 0 : 2 * n].bitcast(FP8X4),
+                scales=hs[:, 0 : 2 * n],
+                in_=groups[k][:, 0 : 8 * n],
             )
-            rg = rg_pool.tile([P, CH, 4], BF16, tag="rg", align_bytes=64)
-            for s in range(n // P):
-                e_sl = slice(s * P, (s + 1) * P)
+            codes[k] = (hc, hs)
+
+        def in_half(h, count):
+            return range((count + 1) // 2) if h == 0 else range((count + 1) // 2, count)
+
+        def messages(k, h):
+            n, ret_out = ROUND_PLAN[k][0], ROUND_PLAN[k][1]
+            hc, hs = codes[k]
+            if h == 0:
+                rets[k] = rg_pool.tile([P, CH * 4], BF16, tag="rg", align_bytes=64, name="rg")
+            rg = rets[k]
+            for s in in_half(h, n // P):
                 ret = pa.tile([P, 4, P], F32, tag="a")
                 for t in range(4):
                     d_sl = slice(t * P, (t + 1) * P)
@@ -279,16 +323,30 @@ def tile_hypergraphgpslayer_pb_t_kernel(
                             start=(g == 0),
                             stop=(g == 1),
                         )
-                leave_psum(ret_out[s], rg[:, e_sl, :], ret[:].rearrange("p t e -> p e t"))
+                leave_psum(
+                    ret_out[s],
+                    rg[:, s * 4 * P : (s + 1) * 4 * P].rearrange("p (e t) -> p e t", t=4),
+                    ret[:].rearrange("p t e -> p e t"),
+                )
+
+        def quantise_ret(k):
+            n = ROUND_PLAN[k][0]
             rc = rg_pool.tile([P, CH], U32, tag="rc", align_bytes=64)
             rsc = rg_pool.tile([P, CH], U8, tag="rsc", align_bytes=64)
             nc.vector.quantize_mx(
-                out=rc[:, 0:n].bitcast(FP8X4),
-                scales=rsc[:, 0:n],
-                in_=rg[:, 0:n, :].rearrange("p c t -> p (c t)"),
+                out=rc[:, 0:n].bitcast(FP8X4), scales=rsc[:, 0:n], in_=rets[k][:, 0 : 4 * n]
             )
-            y = y_pool.tile([P, 4, CH], F32, tag="y")
-            for q in range(4):
+            ret_codes[k] = (rc, rsc)
+
+        ys, obs = {}, {}
+
+        def update(k, h):
+            n, y_out = ROUND_PLAN[k][0], ROUND_PLAN[k][2]
+            rc, rsc = ret_codes[k]
+            if h == 0:
+                ys[k] = ha.tile([P, 4, CH], F32, tag="big", align_bytes=64, name="y")
+            y = ys[k]
+            for q in in_half(h, 4):
                 o_sl = slice(q * P, (q + 1) * P)
                 updT = pb.tile([P, CH], F32, tag="b")
                 nc.tensor.matmul_mx(
@@ -317,8 +375,14 @@ def tile_hypergraphgpslayer_pb_t_kernel(
                         op0=ALU.mult,
                         op1=ALU.add,
                     )
-            ob = ob_pool.tile([P, SUB, DIM], F32, tag="ob")
-            for s in range(n // P):
+
+        def finish(k, h):
+            n, z_out = ROUND_PLAN[k][0], ROUND_PLAN[k][3]
+            y = ys[k]
+            if h == 0:
+                obs[k] = hb.tile([P, SUB, DIM], F32, tag="big", align_bytes=64, name="ob")
+            ob = obs[k]
+            for s in in_half(h, n // P):
                 e_sl = slice(s * P, (s + 1) * P)
                 z = pc.tile([P, DIM], F32, tag="c")
                 nc.tensor.matmul(
@@ -335,9 +399,38 @@ def tile_hypergraphgpslayer_pb_t_kernel(
                         stop=(q == 3),
                     )
                 leave_psum(z_out[s], ob[:, s, :], z[:])
-            if k + 3 < n_rounds:
-                load_x1(k + 3)
-            nc.sync.dma_start(
-                out=out[starts[k] : starts[k] + n, :].rearrange("(s m) o -> m s o", m=P),
-                in_=ob[:, 0 : n // P, :],
-            )
+            if h == 1:
+                nc.sync.dma_start(
+                    out=out[starts[k] : starts[k] + n, :].rearrange("(s m) o -> m s o", m=P),
+                    in_=ob[:, 0 : n // P, :],
+                )
+                if k + 3 < n_rounds:
+                    load_x1(k + 3)
+
+        for k in range(3):
+            load_x1(k)
+        spread(0)
+        for k in range(n_rounds + 4):
+            if k < n_rounds:
+                normalise(k)
+            if k == 1:
+                scale_the_rest()
+            if k + 1 < n_rounds:
+                spread(k + 1)
+            for h in range(2):
+                if 1 <= k <= n_rounds:
+                    messages(k - 1, h)
+                if 3 <= k < n_rounds + 3:
+                    update(k - 3, h)
+                if 4 <= k:
+                    finish(k - 4, h)
+            if k == 0:
+                quantise_x0()
+            if k == 1:
+                quantise_w()
+            if 2 <= k < n_rounds + 2:
+                quantise_ret(k - 2)
+            if k < n_rounds:
+                quantise_h(k)
+            if k == 0:
+                regroup_w()

@@ -123,13 +123,14 @@ def tile_hypergraphgpslayer_pb_t_kernel(
             two = a - a % 2
             return hr[a % 2 - 2][:, two : two + 2, :].rearrange("p a e -> p (a e)").bitcast(BF16)
 
-        def row_sums(a, c0, n, slot, first):
-            nc.vector.tensor_scalar(
-                out=unread(a)[:, c0 : c0 + n],
-                in0=h_raw[a][:, c0 : c0 + n],
-                scalar1=1.0,
-                scalar2=first,
-                op0=ALU.mult,
+        def row_sums(a, c0, n, slot):
+            half = n // 2
+            nc.vector.scalar_tensor_tensor(
+                out=unread(a)[:, c0 : c0 + half],
+                in0=h_raw[a][:, c0 : c0 + half],
+                scalar=TINY,
+                in1=h_raw[a][:, c0 + half : c0 + n],
+                op0=ALU.add,
                 op1=ALU.add,
                 accum_out=dv[:, slot : slot + 1],
             )
@@ -165,8 +166,8 @@ def tile_hypergraphgpslayer_pb_t_kernel(
                 )
 
         for a in range(PLANES - 1):
-            row_sums(a, 0, E, a, TINY)
-        row_sums(7, 0, CUT7, 7, TINY)
+            row_sums(a, 0, E, a)
+        row_sums(7, 0, CUT7, 7)
         de = const.tile([P, E // P], F32)
         nc.vector.tensor_reduce(
             out=de[:], in_=dep[:].rearrange("p a c -> p c a"), axis=AX.X, op=ALU.add

@@ -19,25 +19,25 @@ N_NODES = 1024
 E = 4096
 DIM = 512
 PLANES = 8
-CH = 512
-SUB = CH // P
+CH = 256
+PAIR = 512
+PAIRS = E // PAIR
 TINY = 1e-20
-CUT7 = 2560
-BLOCKS = [(0, 512), (512, 512), (1024, 1024), (2048, 1024), (3072, 1024)]
+
+
+def G_FROM(p):
+    return 7 if p < 3 else 4
+
+CUT7 = 3072
 
 ROUND_PLAN = [
-    (256, "ss", "ssss", "ss"),
-    (256, "ss", "ssss", "ss"),
-    (512, "ssss", "ssss", "ssss"),
-    (512, "ssss", "ssss", "ssss"),
-    (512, "ssss", "ssss", "ssss"),
-    (512, "ssss", "ssss", "ssss"),
-    (512, "ssss", "ssss", "ssss"),
-    (512, "ssss", "ssss", "ssss"),
-    (256, "ss", "ssss", "sv"),
-    (128, "s", "ssvv", "s"),
-    (128, "v", "svsv", "v"),
-]
+    (256, 0, "ss", "ssss", "ss"),
+    (256, 1, "ss", "ssss", "ss"),
+] * 7 + [
+    (128, 0, "s", "ssss", "s"),
+    (128, 1, "s", "ssss", "s"),
+] * 2
+
 
 FLOPS = 2 * E * N_NODES * DIM + 2 * E * DIM * DIM
 
@@ -48,7 +48,8 @@ def tile_hypergraphgpslayer_pb_t_kernel(
     nc = tc.nc
     with ExitStack() as ctx:
         const = ctx.enter_context(tc.tile_pool(name="const", bufs=1))
-        ha = ctx.enter_context(tc.tile_pool(name="ha", bufs=4))
+        hr_pool = ctx.enter_context(tc.tile_pool(name="hr", bufs=PAIRS))
+        ha = ctx.enter_context(tc.tile_pool(name="ha", bufs=5))
         hb = ctx.enter_context(tc.tile_pool(name="hb", bufs=4))
         hq_pool = ctx.enter_context(tc.tile_pool(name="hq", bufs=2))
         rg_pool = ctx.enter_context(tc.tile_pool(name="rg", bufs=2))
@@ -60,9 +61,6 @@ def tile_hypergraphgpslayer_pb_t_kernel(
 
         gate_b = const.tile([P, 1], BF16)
         nc.scalar.dma_start(out=gate_b[:], in_=gate_return.partition_broadcast(P))
-        br_c = const.tile([P, 4], BF16)
-        with nc.allow_non_contiguous_dma(reason="512 bias values, one to a partition and column"):
-            nc.scalar.dma_start(out=br_c[:], in_=br.rearrange("(q p) -> p q", p=P))
 
         h_dram = incidence_1.rearrange("(g p j) e -> p g j e", g=2, j=4)
         h_raw = []
@@ -84,6 +82,9 @@ def tile_hypergraphgpslayer_pb_t_kernel(
         wraw = wst[:, 0].rearrange("p (t o) -> p t o", t=4)
         nc.sync.dma_start(out=wraw, in_=Wr.rearrange("(p t) o -> p t o", t=4))
 
+        br_b = const.tile([P, DIM], BF16)
+        nc.sync.dma_start(out=br_b[:], in_=br.partition_broadcast(P))
+
         ident = const.tile([P, P], F32)
         make_identity(nc, ident[:])
         ident_bf = const.tile([P, P], BF16)
@@ -99,24 +100,21 @@ def tile_hypergraphgpslayer_pb_t_kernel(
         nc.scalar.activation(
             out=warm[:], in_=g_col[:], func=ACT.Abs_reciprocal_sqrt, bias=1.0, scale=0.0
         )
-        gbr = const.tile([P, 4], F32)
-        nc.scalar.activation(out=gbr[:], in_=br_c[:], func=ACT.Copy, scale=g_col[:, 0:1])
 
         ctx.enter_context(
             tc.manual_schedule(
-                engines={mybir.EngineType.DVE, mybir.EngineType.Activation, mybir.EngineType.PE}
+                engines={
+                    mybir.EngineType.DVE,
+                    mybir.EngineType.Activation,
+                    mybir.EngineType.PE,
+                    mybir.EngineType.Pool,
+                }
             )
         )
 
         dv = const.tile([P, PLANES + 1], F32)
         rv = const.tile([P, PLANES], F32)
-        hr = [
-            const.tile([P, PLANES, n], F32, name="hr%d" % b) for b, (c0, n) in enumerate(BLOCKS)
-        ]
-
-        def block_of(c0):
-            return max(b for b in range(len(BLOCKS)) if BLOCKS[b][0] <= c0)
-
+        hr = [hr_pool.tile([P, PLANES, PAIR], F32, tag="hr", name="hr_p") for p in range(PAIRS)]
         dep = pc.tile([P, PLANES, E // P], F32, tag="c")
 
         def unread(a):
@@ -126,7 +124,7 @@ def tile_hypergraphgpslayer_pb_t_kernel(
         def row_sums(a, c0, n, slot):
             half = n // 2
             nc.vector.scalar_tensor_tensor(
-                out=unread(a)[:, c0 : c0 + half],
+                out=unread(a)[:, 0:half],
                 in0=h_raw[a][:, c0 : c0 + half],
                 scalar=TINY,
                 in1=h_raw[a][:, c0 + half : c0 + n],
@@ -141,19 +139,16 @@ def tile_hypergraphgpslayer_pb_t_kernel(
             )
 
         def scale_rows(engine, a, c0, c1):
-            while c0 < c1:
-                b = block_of(c0)
-                first = BLOCKS[b][0]
-                c = min(c1, first + BLOCKS[b][1])
-                dst = hr[b][:, a, c0 - first : c - first]
-                src, by = h_raw[a][:, c0:c], rv[:, a : a + 1]
+            step = PAIR if engine == "s" else PAIR // 2
+            for c in range(c0, c1, step):
+                dst = hr[c // PAIR][:, a, c % PAIR : c % PAIR + step]
+                src, by = h_raw[a][:, c : c + step], rv[:, a : a + 1]
                 if engine == "s":
                     nc.scalar.activation(out=dst, in_=src, func=ACT.Copy, scale=by)
                 else:
                     nc.gpsimd.tensor_scalar(
                         out=dst, in0=src, scalar1=by, scalar2=0.0, op0=ALU.mult, op1=ALU.add
                     )
-                c0 = c
 
         for a, c0, n in pieces:
             for c in range(c0 // P, (c0 + n) // P):
@@ -174,39 +169,50 @@ def tile_hypergraphgpslayer_pb_t_kernel(
         )
         rs = const.tile([P, E // P], F32)
 
-        for a in (0, 2):
+        for a in range(3):
             inverse_root(a)
-            scale_rows("s", a, 0, E // 2)
-            inverse_root(a + 1)
-            scale_rows("s", a, E // 2, E)
-        inverse_root(4)
-        scale_rows("s", 4, 0, E // 2)
-        inverse_root(5)
-        scale_rows("s", 4, E // 2, 3 * E // 4)
+            scale_rows("s", a, 0, E)
+        inverse_root(3)
         nc.scalar.activation(
-            out=unread(7)[:, CUT7:],
+            out=hr[-3][:, 6:8, :].rearrange("p a e -> p (a e)").bitcast(BF16)[:, 0 : E - CUT7],
             in_=h_raw[7][:, CUT7:],
             func=ACT.Copy,
             accum_out=dv[:, 8:9],
         )
-        inverse_root(6)
         nc.scalar.activation(
             out=rs[:], in_=de[:], func=ACT.Abs_reciprocal_sqrt, bias=tiny[:, 0:1]
         )
+        for a in range(4, 7):
+            inverse_root(a)
         inverse_root(7, dv[:, 8:9])
-        scale_rows("s", 6, 0, CH)
-        scale_rows("s", 7, 0, CH)
-        for a in (1, 3, 5):
-            scale_rows("g", a, 0, E)
+        for a in (3, 4, 5, 6, 7):
+            scale_rows("s", a, 0, PAIR)
 
-        def scale_the_rest():
-            scale_rows("s", 6, CH, 1024)
-            scale_rows("s", 4, 3 * E // 4, E)
-            scale_rows("s", 6, 1024, E // 2)
-            for c in range(CH, E, CH):
-                scale_rows("g", 7, c, c + CH)
-                if c >= E // 2:
-                    scale_rows("g", 6, c, c + CH)
+        gbr_b = const.tile([P, DIM], F32)
+        gbr = const.tile([P, 4], F32)
+
+        def scale_pair(p):
+            c0 = p * PAIR
+            for a in range(4, PLANES):
+                scale_rows("g" if a > G_FROM(p) else "s", a, c0, c0 + PAIR)
+
+        def bias_row():
+            nc.gpsimd.tensor_scalar(
+                out=gbr_b[:],
+                in0=br_b[:],
+                scalar1=g_col[:, 0:1],
+                scalar2=0.0,
+                op0=ALU.mult,
+                op1=ALU.add,
+            )
+            turned = pb.tile([P, 4, P], F32, tag="b")
+            for q in range(4):
+                nc.tensor.transpose(
+                    out=turned[:, q, :],
+                    in_=gbr_b[:, q * P : (q + 1) * P],
+                    identity=ident[:],
+                )
+            nc.scalar.copy(out=gbr[:], in_=turned[:, :, 0])
 
         x0g = ha.tile([P, 2, DIM, 4], BF16, tag="big", align_bytes=64)
         for g in range(2):
@@ -237,16 +243,15 @@ def tile_hypergraphgpslayer_pb_t_kernel(
 
         starts = [sum(plan[0] for plan in ROUND_PLAN[:k]) for k in range(len(ROUND_PLAN))]
         n_rounds = len(ROUND_PLAN)
-        x1_tiles, spreads, groups, codes, rets, ret_codes = {}, {}, {}, {}, {}, {}
+        x1_tiles, spreads, groups, codes, rets, ret_codes, ys, obs = {}, {}, {}, {}, {}, {}, {}, {}
 
-        def load_x1(k):
-            n = ROUND_PLAN[k][0]
-            x1t = x1_pool.tile([P, SUB, DIM], BF16, tag="x1")
+        def load_x1(p):
+            x1t = x1_pool.tile([P, PAIR // P, DIM], BF16, tag="x1")
             nc.sync.dma_start(
-                out=x1t[:, 0 : n // P, :],
-                in_=x_1_new[starts[k] : starts[k] + n, :].rearrange("(s m) o -> m s o", m=P),
+                out=x1t[:],
+                in_=x_1_new[p * PAIR : (p + 1) * PAIR, :].rearrange("(s m) o -> m s o", m=P),
             )
-            x1_tiles[k] = x1t
+            x1_tiles[p] = x1t
 
         def leave_psum(engine, dst, src):
             if engine == "s":
@@ -254,26 +259,24 @@ def tile_hypergraphgpslayer_pb_t_kernel(
             else:
                 nc.vector.tensor_copy(out=dst, in_=src)
 
-        def spread(k):
-            n = ROUND_PLAN[k][0]
-            sp = ps.tile([P, CH], F32, tag="s")
-            for q in range(n // P):
-                c = starts[k] // P + q
+        def spread(p):
+            sp = ps.tile([P, PAIR], F32, tag="s")
+            for q in range(PAIR // P):
+                c = p * PAIR // P + q
                 nc.tensor.transpose(
                     out=sp[:, q * P : (q + 1) * P],
                     in_=rs[:, c : c + 1].to_broadcast([P, P]),
                     identity=ident[:],
                 )
-            spreads[k] = sp
+            spreads[p] = sp
 
         def normalise(k):
             n = ROUND_PLAN[k][0]
-            b = block_of(starts[k])
-            c0 = starts[k] - BLOCKS[b][0]
+            p, d0 = divmod(starts[k], PAIR)
             hg = ha.tile([P, 2 * CH * 4], BF16, tag="big", align_bytes=64)
             hgv = hg[:, 0 : 8 * n].rearrange("p (g c i t) -> p g c t i", g=2, i=2, t=4)
             by = (
-                spreads[k][:, 0:n]
+                spreads[p][:, d0 : d0 + n]
                 .rearrange("p (c i) -> p c i", i=2)
                 .unsqueeze(2)
                 .to_broadcast([P, n // 2, 4, 2])
@@ -281,7 +284,7 @@ def tile_hypergraphgpslayer_pb_t_kernel(
             for g in range(2):
                 nc.vector.tensor_tensor(
                     out=hgv[:, g],
-                    in0=hr[b][:, 4 * g : 4 * g + 4, c0 : c0 + n].rearrange(
+                    in0=hr[p][:, 4 * g : 4 * g + 4, d0 : d0 + n].rearrange(
                         "p t (c i) -> p c t i", i=2
                     ),
                     in1=by,
@@ -304,7 +307,7 @@ def tile_hypergraphgpslayer_pb_t_kernel(
             return range((count + 1) // 2) if h == 0 else range((count + 1) // 2, count)
 
         def messages(k, h):
-            n, ret_out = ROUND_PLAN[k][0], ROUND_PLAN[k][1]
+            n, ret_out = ROUND_PLAN[k][0], ROUND_PLAN[k][2]
             hc, hs = codes[k]
             if h == 0:
                 rets[k] = rg_pool.tile([P, CH * 4], BF16, tag="rg", align_bytes=64, name="rg")
@@ -339,19 +342,65 @@ def tile_hypergraphgpslayer_pb_t_kernel(
             )
             ret_codes[k] = (rc, rsc)
 
-        ys, obs = {}, {}
+        def out_rows(k, s):
+            p, d0 = divmod(starts[k] + s * P, PAIR)
+            return p, d0 // P
+
+        def bias_residual(k):
+            n, direct = ROUND_PLAN[k][0], ROUND_PLAN[k][1]
+            p = starts[k] // PAIR
+            if p not in obs:
+                obs[p] = hr_pool.tile([P, PAIR // P, DIM], F32, tag="hr", name="ob")
+            for s in range(n // P - direct, n // P):
+                p, row = out_rows(k, s)
+                for c in range(0, DIM, P):
+                    nc.gpsimd.tensor_tensor(
+                        out=obs[p][:, row, c : c + P],
+                        in0=x1_tiles[p][:, row, c : c + P],
+                        in1=gbr_b[:, c : c + P],
+                        op=ALU.add,
+                    )
+
+        def update_direct(k):
+            n, direct = ROUND_PLAN[k][0], ROUND_PLAN[k][1]
+            rc, rsc = ret_codes[k]
+            for s in range(n // P - direct, n // P):
+                e_sl = slice(s * P, (s + 1) * P)
+                p, row = out_rows(k, s)
+                upd = pc.tile([P, DIM], F32, tag="c")
+                nc.tensor.matmul_mx(
+                    out=upd[:],
+                    lhsT=rc[:, e_sl].bitcast(FP8X4),
+                    lhsT_scale=rsc[:, e_sl],
+                    rhs=wc[:].bitcast(FP8X4),
+                    rhs_scale=ws[:],
+                    start=True,
+                    stop=True,
+                )
+                nc.vector.scalar_tensor_tensor(
+                    out=obs[p][:, row, :],
+                    in0=upd[:],
+                    scalar=g_col[:, 0:1],
+                    in1=obs[p][:, row, :],
+                    op0=ALU.mult,
+                    op1=ALU.add,
+                )
 
         def update(k, h):
-            n, y_out = ROUND_PLAN[k][0], ROUND_PLAN[k][2]
+            n, direct, y_out = ROUND_PLAN[k][0], ROUND_PLAN[k][1], ROUND_PLAN[k][3]
+            n -= direct * P
+            if n == 0:
+                return
             rc, rsc = ret_codes[k]
             if h == 0:
                 ys[k] = ha.tile([P, 4, CH], F32, tag="big", align_bytes=64, name="y")
             y = ys[k]
-            for q in in_half(h, 4):
+            updT = pb.tile([P, 2, CH], F32, tag="b")
+            for i in range(2):
+                q = 2 * h + i
                 o_sl = slice(q * P, (q + 1) * P)
-                updT = pb.tile([P, CH], F32, tag="b")
                 nc.tensor.matmul_mx(
-                    out=updT[:, 0:n],
+                    out=updT[:, i, 0:n],
                     lhsT=wc[:, o_sl].bitcast(FP8X4),
                     lhsT_scale=ws[:, o_sl],
                     rhs=rc[:, 0:n].bitcast(FP8X4),
@@ -359,10 +408,12 @@ def tile_hypergraphgpslayer_pb_t_kernel(
                     start=True,
                     stop=True,
                 )
+            for i in range(2):
+                q = 2 * h + i
                 if y_out[q] == "s":
                     nc.scalar.activation(
                         out=y[:, q, 0:n],
-                        in_=updT[:, 0:n],
+                        in_=updT[:, i, 0:n],
                         func=ACT.Identity,
                         bias=gbr[:, q : q + 1],
                         scale=g_col[:, 0:1],
@@ -370,68 +421,100 @@ def tile_hypergraphgpslayer_pb_t_kernel(
                 else:
                     nc.vector.tensor_scalar(
                         out=y[:, q, 0:n],
-                        in0=updT[:, 0:n],
+                        in0=updT[:, i, 0:n],
                         scalar1=g_col[:, 0:1],
                         scalar2=gbr[:, q : q + 1],
                         op0=ALU.mult,
                         op1=ALU.add,
                     )
 
+        def store(e0, n):
+            p, d0 = divmod(e0, PAIR)
+            nc.sync.dma_start(
+                out=out[e0 : e0 + n, :].rearrange("(s m) o -> m s o", m=P),
+                in_=obs[p][:, d0 // P : (d0 + n) // P, :],
+            )
+
         def finish(k, h):
-            n, z_out = ROUND_PLAN[k][0], ROUND_PLAN[k][3]
-            y = ys[k]
-            if h == 0:
-                obs[k] = hb.tile([P, SUB, DIM], F32, tag="big", align_bytes=64, name="ob")
-            ob = obs[k]
+            n, direct, z_out = ROUND_PLAN[k][0], ROUND_PLAN[k][1], ROUND_PLAN[k][4]
             for s in in_half(h, n // P):
-                e_sl = slice(s * P, (s + 1) * P)
+                if s >= n // P - direct:
+                    continue
+                p, row = out_rows(k, s)
                 z = pc.tile([P, DIM], F32, tag="c")
                 nc.tensor.matmul(
-                    out=z[:], lhsT=ident_bf[:], rhs=x1_tiles[k][:, s, :], start=True, stop=False
+                    out=z[:], lhsT=ident_bf[:], rhs=x1_tiles[p][:, row, :], start=True, stop=False
                 )
                 for q in range(4):
-                    o_sl = slice(q * P, (q + 1) * P)
                     nc.tensor.matmul(
-                        out=z[:, o_sl],
-                        lhsT=y[:, q, e_sl],
+                        out=z[:, q * P : (q + 1) * P],
+                        lhsT=ys[k][:, q, s * P : (s + 1) * P],
                         rhs=ident[:],
                         is_transpose=True,
                         start=False,
                         stop=(q == 3),
                     )
-                leave_psum(z_out[s], ob[:, s, :], z[:])
-            if h == 1:
-                nc.sync.dma_start(
-                    out=out[starts[k] : starts[k] + n, :].rearrange("(s m) o -> m s o", m=P),
-                    in_=ob[:, 0 : n // P, :],
-                )
-                if k + 3 < n_rounds:
-                    load_x1(k + 3)
+                leave_psum(z_out[s], obs[p][:, row, :], z[:])
+            p = starts[k] // PAIR
+            if h == 1 and p == PAIRS - 1:
+                store(starts[k], n)
+            elif h == 1 and (starts[k] + n) % PAIR == 0:
+                store(p * PAIR, PAIR)
+                if p + 3 < PAIRS:
+                    load_x1(p + 3)
 
-        for k in range(3):
-            load_x1(k)
+        def update_both(k):
+            update(k, 0)
+            update_direct(k)
+            update(k, 1)
+
+        def finish_both(k):
+            finish(k, 0)
+            finish(k, 1)
+
+        for p in range(3):
+            load_x1(p)
         spread(0)
-        for k in range(n_rounds + 4):
-            if k < n_rounds:
-                normalise(k)
-            if k == 1:
-                scale_the_rest()
-            if k + 1 < n_rounds:
-                spread(k + 1)
+        for k in range(n_rounds):
+            normalise(k)
+            if k == 0:
+                scale_rows("s", 3, PAIR, E)
+                scale_pair(1)
+                bias_row()
+            else:
+                bias_residual(k - 1)
+            if k < PAIRS - 2:
+                scale_pair(k + 2)
+            if k + 1 < n_rounds and starts[k + 1] % PAIR == 0:
+                spread(starts[k + 1] // PAIR)
             for h in range(2):
-                if 1 <= k <= n_rounds:
+                if k >= 1:
                     messages(k - 1, h)
-                if 3 <= k < n_rounds + 3:
+                if k >= 3:
                     update(k - 3, h)
-                if 4 <= k:
+                    if h == 0:
+                        update_direct(k - 3)
+                if k >= 4:
                     finish(k - 4, h)
             if k == 0:
                 quantise_x0()
             if k == 1:
                 quantise_w()
-            if 2 <= k < n_rounds + 2:
+            if k >= 2:
                 quantise_ret(k - 2)
-            if k < n_rounds:
-                quantise_h(k)
+            quantise_h(k)
             if k == 0:
                 regroup_w()
+        bias_residual(n_rounds - 1)
+        last = n_rounds - 1
+        for h in range(2):
+            messages(last, h)
+        quantise_ret(last - 1)
+        update_both(last - 2)
+        finish_both(last - 3)
+        quantise_ret(last)
+        update_both(last - 1)
+        finish_both(last - 2)
+        update_both(last)
+        finish_both(last - 1)
+        finish_both(last)

@@ -23,20 +23,15 @@ CH = 256
 PAIR = 512
 PAIRS = E // PAIR
 TINY = 1e-20
+LATE = ((5, "v"), (6, "v")), ((7, "v"), (4, "s"))
 
 
 def G_FROM(p):
-    return 7 if p < 3 else 4
+    return 7
 
 CUT7 = 3072
 
-ROUND_PLAN = [
-    (256, 0, "ss", "ssss", "ss"),
-    (256, 1, "ss", "ssss", "ss"),
-] * 7 + [
-    (128, 0, "s", "ssss", "s"),
-    (128, 1, "s", "ssss", "s"),
-] * 2
+ROUND_PLAN = [(256, 0, "ss", "ssss", "ss")] * 14 + [(128, 0, "s", "ssvv", "s")] * 4
 
 
 FLOPS = 2 * E * N_NODES * DIM + 2 * E * DIM * DIM
@@ -139,12 +134,14 @@ def tile_hypergraphgpslayer_pb_t_kernel(
             )
 
         def scale_rows(engine, a, c0, c1):
-            step = PAIR if engine == "s" else PAIR // 2
+            step = PAIR if engine != "g" else PAIR // 2
             for c in range(c0, c1, step):
                 dst = hr[c // PAIR][:, a, c % PAIR : c % PAIR + step]
                 src, by = h_raw[a][:, c : c + step], rv[:, a : a + 1]
                 if engine == "s":
                     nc.scalar.activation(out=dst, in_=src, func=ACT.Copy, scale=by)
+                elif engine == "v":
+                    nc.vector.tensor_scalar_mul(out=dst, in0=src, scalar1=by)
                 else:
                     nc.gpsimd.tensor_scalar(
                         out=dst, in0=src, scalar1=by, scalar2=0.0, op0=ALU.mult, op1=ALU.add
@@ -435,16 +432,18 @@ def tile_hypergraphgpslayer_pb_t_kernel(
                 in_=obs[p][:, d0 // P : (d0 + n) // P, :],
             )
 
-        def finish(k, h):
+        def finish(k):
             n, direct, z_out = ROUND_PLAN[k][0], ROUND_PLAN[k][1], ROUND_PLAN[k][4]
-            for s in in_half(h, n // P):
-                if s >= n // P - direct:
-                    continue
+            banks = []
+            for s in range(n // P - direct):
                 p, row = out_rows(k, s)
                 z = pc.tile([P, DIM], F32, tag="c")
                 nc.tensor.matmul(
                     out=z[:], lhsT=ident_bf[:], rhs=x1_tiles[p][:, row, :], start=True, stop=False
                 )
+                banks.append(z)
+            for s, z in enumerate(banks):
+                p, row = out_rows(k, s)
                 for q in range(4):
                     nc.tensor.matmul(
                         out=z[:, q * P : (q + 1) * P],
@@ -456,21 +455,23 @@ def tile_hypergraphgpslayer_pb_t_kernel(
                     )
                 leave_psum(z_out[s], obs[p][:, row, :], z[:])
             p = starts[k] // PAIR
-            if h == 1 and p == PAIRS - 1:
+            if p == PAIRS - 1:
                 store(starts[k], n)
-            elif h == 1 and (starts[k] + n) % PAIR == 0:
+            elif (starts[k] + n) % PAIR == 0:
                 store(p * PAIR, PAIR)
                 if p + 3 < PAIRS:
                     load_x1(p + 3)
+
+        def late_scale(k):
+            p = k // 2 + 2
+            if p < PAIRS:
+                for a, engine in LATE[k % 2]:
+                    scale_rows(engine, a, p * PAIR, (p + 1) * PAIR)
 
         def update_both(k):
             update(k, 0)
             update_direct(k)
             update(k, 1)
-
-        def finish_both(k):
-            finish(k, 0)
-            finish(k, 1)
 
         for p in range(3):
             load_x1(p)
@@ -483,19 +484,16 @@ def tile_hypergraphgpslayer_pb_t_kernel(
                 bias_row()
             else:
                 bias_residual(k - 1)
-            if k < PAIRS - 2:
-                scale_pair(k + 2)
+            late_scale(k)
             if k + 1 < n_rounds and starts[k + 1] % PAIR == 0:
                 spread(starts[k + 1] // PAIR)
-            for h in range(2):
-                if k >= 1:
-                    messages(k - 1, h)
-                if k >= 3:
-                    update(k - 3, h)
-                    if h == 0:
-                        update_direct(k - 3)
-                if k >= 4:
-                    finish(k - 4, h)
+            if k >= 1:
+                messages(k - 1, 0)
+                messages(k - 1, 1)
+            if k >= 3:
+                update_both(k - 3)
+            if k >= 4:
+                finish(k - 4)
             if k == 0:
                 quantise_x0()
             if k == 1:
@@ -511,10 +509,10 @@ def tile_hypergraphgpslayer_pb_t_kernel(
             messages(last, h)
         quantise_ret(last - 1)
         update_both(last - 2)
-        finish_both(last - 3)
+        finish(last - 3)
         quantise_ret(last)
         update_both(last - 1)
-        finish_both(last - 2)
+        finish(last - 2)
         update_both(last)
-        finish_both(last - 1)
-        finish_both(last)
+        finish(last - 1)
+        finish(last)

@@ -23,15 +23,19 @@ CH = 256
 PAIR = 512
 PAIRS = E // PAIR
 TINY = 1e-20
-LATE = ((5, "v"), (6, "v")), ((7, "v"), (4, "s"))
+LATE = ((4, "g"), (5, "g")), ((6, "g"), (7, "g"))
 
 
 def G_FROM(p):
     return 7
 
-CUT7 = 3072
+CUT7 = 2560
 
-ROUND_PLAN = [(256, 0, "ss", "ssss", "ss")] * 14 + [(128, 0, "s", "ssvv", "s")] * 4
+ROUND_PLAN = (
+    [(256, "ss", "ssss", "ss"), (256, "ss", "ssss", "ss"), (256, "ss", "ssss", "sv")] * 4
+    + [(256, "ss", "ssss", "sv")] * 2
+    + [(128, "s", "svsv", "v")] * 4
+)
 
 
 FLOPS = 2 * E * N_NODES * DIM + 2 * E * DIM * DIM
@@ -134,7 +138,7 @@ def tile_hypergraphgpslayer_pb_t_kernel(
             )
 
         def scale_rows(engine, a, c0, c1):
-            step = PAIR if engine != "g" else PAIR // 2
+            step = PAIR
             for c in range(c0, c1, step):
                 dst = hr[c // PAIR][:, a, c % PAIR : c % PAIR + step]
                 src, by = h_raw[a][:, c : c + step], rv[:, a : a + 1]
@@ -166,9 +170,11 @@ def tile_hypergraphgpslayer_pb_t_kernel(
         )
         rs = const.tile([P, E // P], F32)
 
-        for a in range(3):
+        for a in range(2):
             inverse_root(a)
             scale_rows("s", a, 0, E)
+        inverse_root(2)
+        scale_rows("s", 2, 0, 3072)
         inverse_root(3)
         nc.scalar.activation(
             out=hr[-3][:, 6:8, :].rearrange("p a e -> p (a e)").bitcast(BF16)[:, 0 : E - CUT7],
@@ -304,7 +310,7 @@ def tile_hypergraphgpslayer_pb_t_kernel(
             return range((count + 1) // 2) if h == 0 else range((count + 1) // 2, count)
 
         def messages(k, h):
-            n, ret_out = ROUND_PLAN[k][0], ROUND_PLAN[k][2]
+            n, ret_out = ROUND_PLAN[k][0], ROUND_PLAN[k][1]
             hc, hs = codes[k]
             if h == 0:
                 rets[k] = rg_pool.tile([P, CH * 4], BF16, tag="rg", align_bytes=64, name="rg")
@@ -343,51 +349,8 @@ def tile_hypergraphgpslayer_pb_t_kernel(
             p, d0 = divmod(starts[k] + s * P, PAIR)
             return p, d0 // P
 
-        def bias_residual(k):
-            n, direct = ROUND_PLAN[k][0], ROUND_PLAN[k][1]
-            p = starts[k] // PAIR
-            if p not in obs:
-                obs[p] = hr_pool.tile([P, PAIR // P, DIM], F32, tag="hr", name="ob")
-            for s in range(n // P - direct, n // P):
-                p, row = out_rows(k, s)
-                for c in range(0, DIM, P):
-                    nc.gpsimd.tensor_tensor(
-                        out=obs[p][:, row, c : c + P],
-                        in0=x1_tiles[p][:, row, c : c + P],
-                        in1=gbr_b[:, c : c + P],
-                        op=ALU.add,
-                    )
-
-        def update_direct(k):
-            n, direct = ROUND_PLAN[k][0], ROUND_PLAN[k][1]
-            rc, rsc = ret_codes[k]
-            for s in range(n // P - direct, n // P):
-                e_sl = slice(s * P, (s + 1) * P)
-                p, row = out_rows(k, s)
-                upd = pc.tile([P, DIM], F32, tag="c")
-                nc.tensor.matmul_mx(
-                    out=upd[:],
-                    lhsT=rc[:, e_sl].bitcast(FP8X4),
-                    lhsT_scale=rsc[:, e_sl],
-                    rhs=wc[:].bitcast(FP8X4),
-                    rhs_scale=ws[:],
-                    start=True,
-                    stop=True,
-                )
-                nc.vector.scalar_tensor_tensor(
-                    out=obs[p][:, row, :],
-                    in0=upd[:],
-                    scalar=g_col[:, 0:1],
-                    in1=obs[p][:, row, :],
-                    op0=ALU.mult,
-                    op1=ALU.add,
-                )
-
         def update(k, h):
-            n, direct, y_out = ROUND_PLAN[k][0], ROUND_PLAN[k][1], ROUND_PLAN[k][3]
-            n -= direct * P
-            if n == 0:
-                return
+            n, y_out = ROUND_PLAN[k][0], ROUND_PLAN[k][2]
             rc, rsc = ret_codes[k]
             if h == 0:
                 ys[k] = ha.tile([P, 4, CH], F32, tag="big", align_bytes=64, name="y")
@@ -425,6 +388,8 @@ def tile_hypergraphgpslayer_pb_t_kernel(
                         op1=ALU.add,
                     )
 
+        held, to_store = [], []
+
         def store(e0, n):
             p, d0 = divmod(e0, PAIR)
             nc.sync.dma_start(
@@ -433,14 +398,22 @@ def tile_hypergraphgpslayer_pb_t_kernel(
             )
 
         def finish(k):
-            n, direct, z_out = ROUND_PLAN[k][0], ROUND_PLAN[k][1], ROUND_PLAN[k][4]
+            n, z_out = ROUND_PLAN[k][0], ROUND_PLAN[k][3]
+            p = starts[k] // PAIR
+            if p not in obs:
+                obs[p] = hr_pool.tile([P, PAIR // P, DIM], F32, tag="hr", name="ob")
             banks = []
-            for s in range(n // P - direct):
+            for s in range(n // P):
                 p, row = out_rows(k, s)
                 z = pc.tile([P, DIM], F32, tag="c")
-                nc.tensor.matmul(
-                    out=z[:], lhsT=ident_bf[:], rhs=x1_tiles[p][:, row, :], start=True, stop=False
-                )
+                if z_out[s] == "s":
+                    nc.tensor.matmul(
+                        out=z[:],
+                        lhsT=ident_bf[:],
+                        rhs=x1_tiles[p][:, row, :],
+                        start=True,
+                        stop=False,
+                    )
                 banks.append(z)
             for s, z in enumerate(banks):
                 p, row = out_rows(k, s)
@@ -450,17 +423,33 @@ def tile_hypergraphgpslayer_pb_t_kernel(
                         lhsT=ys[k][:, q, s * P : (s + 1) * P],
                         rhs=ident[:],
                         is_transpose=True,
-                        start=False,
-                        stop=(q == 3),
+                        start=(z_out[s] == "v"),
+                        stop=(z_out[s] == "v" or q == 3),
                     )
-                leave_psum(z_out[s], obs[p][:, row, :], z[:])
-            p = starts[k] // PAIR
+                if z_out[s] == "s":
+                    nc.scalar.copy(out=obs[p][:, row, :], in_=z[:])
+                else:
+                    held.append((obs[p][:, row, :], z[:], x1_tiles[p][:, row, :]))
             if p == PAIRS - 1:
-                store(starts[k], n)
+                to_store.append((starts[k], n))
             elif (starts[k] + n) % PAIR == 0:
-                store(p * PAIR, PAIR)
+                to_store.append((p * PAIR, PAIR))
                 if p + 3 < PAIRS:
                     load_x1(p + 3)
+            if not held:
+                empty_held()
+
+        def empty_held():
+            for dst, src, residual in held:
+                nc.vector.tensor_tensor(out=dst, in0=src, in1=residual, op=ALU.add)
+            for e0, n in to_store:
+                store(e0, n)
+            held.clear()
+            to_store.clear()
+
+        def pace(k):
+            seen = const.tile([P, 1], U32, tag="seen")
+            nc.gpsimd.tensor_copy(out=seen[:], in_=codes[k][0][:, 0:1])
 
         def late_scale(k):
             p = k // 2 + 2
@@ -470,7 +459,6 @@ def tile_hypergraphgpslayer_pb_t_kernel(
 
         def update_both(k):
             update(k, 0)
-            update_direct(k)
             update(k, 1)
 
         for p in range(3):
@@ -478,12 +466,14 @@ def tile_hypergraphgpslayer_pb_t_kernel(
         spread(0)
         for k in range(n_rounds):
             normalise(k)
+            empty_held()
             if k == 0:
                 scale_rows("s", 3, PAIR, E)
                 scale_pair(1)
+                scale_rows("s", 2, 3072, E)
                 bias_row()
             else:
-                bias_residual(k - 1)
+                pace(k - 1)
             late_scale(k)
             if k + 1 < n_rounds and starts[k + 1] % PAIR == 0:
                 spread(starts[k + 1] // PAIR)
@@ -503,16 +493,20 @@ def tile_hypergraphgpslayer_pb_t_kernel(
             quantise_h(k)
             if k == 0:
                 regroup_w()
-        bias_residual(n_rounds - 1)
         last = n_rounds - 1
+        empty_held()
         for h in range(2):
             messages(last, h)
         quantise_ret(last - 1)
         update_both(last - 2)
         finish(last - 3)
         quantise_ret(last)
+        empty_held()
         update_both(last - 1)
         finish(last - 2)
+        empty_held()
         update_both(last)
         finish(last - 1)
+        empty_held()
         finish(last)
+        empty_held()

@@ -23,18 +23,16 @@ CH = 256
 PAIR = 512
 PAIRS = E // PAIR
 TINY = 1e-20
-LATE = ((4, "g"), (5, "g")), ((6, "g"), (7, "g"))
+EARLY2 = 1536
+BY_S = ((7, 4), (7, 5), (7, 6), (7, 7))
 
-
-def G_FROM(p):
-    return 7
 
 CUT7 = 2560
 
 ROUND_PLAN = (
     [(256, "ss", "ssss", "ss"), (256, "ss", "ssss", "ss"), (256, "ss", "ssss", "sv")] * 4
     + [(256, "ss", "ssss", "sv")] * 2
-    + [(128, "s", "svsv", "v")] * 4
+    + [(128, "s", "ssss", "s")] * 4
 )
 
 
@@ -48,11 +46,11 @@ def tile_hypergraphgpslayer_pb_t_kernel(
     with ExitStack() as ctx:
         const = ctx.enter_context(tc.tile_pool(name="const", bufs=1))
         hr_pool = ctx.enter_context(tc.tile_pool(name="hr", bufs=PAIRS))
-        ha = ctx.enter_context(tc.tile_pool(name="ha", bufs=5))
+        ha = ctx.enter_context(tc.tile_pool(name="ha", bufs=6))
         hb = ctx.enter_context(tc.tile_pool(name="hb", bufs=4))
         hq_pool = ctx.enter_context(tc.tile_pool(name="hq", bufs=2))
         rg_pool = ctx.enter_context(tc.tile_pool(name="rg", bufs=2))
-        x1_pool = ctx.enter_context(tc.tile_pool(name="x1", bufs=3))
+        x1_pool = ctx.enter_context(tc.tile_pool(name="x1", bufs=2))
         ps = ctx.enter_context(tc.psum_pool(name="ps", bufs=2))
         pa = ctx.enter_context(tc.psum_pool(name="pa", bufs=2))
         pb = ctx.enter_context(tc.psum_pool(name="pb", bufs=2))
@@ -81,7 +79,7 @@ def tile_hypergraphgpslayer_pb_t_kernel(
         wraw = wst[:, 0].rearrange("p (t o) -> p t o", t=4)
         nc.sync.dma_start(out=wraw, in_=Wr.rearrange("(p t) o -> p t o", t=4))
 
-        br_b = const.tile([P, DIM], BF16)
+        br_b = rg_pool.tile([P, DIM], BF16, tag="rg", align_bytes=64)
         nc.sync.dma_start(out=br_b[:], in_=br.partition_broadcast(P))
 
         ident = const.tile([P, P], F32)
@@ -170,12 +168,17 @@ def tile_hypergraphgpslayer_pb_t_kernel(
         )
         rs = const.tile([P, E // P], F32)
 
+        inverse_root(0)
         for a in range(2):
-            inverse_root(a)
-            scale_rows("s", a, 0, E)
-        inverse_root(2)
-        scale_rows("s", 2, 0, 3072)
+            scale_rows("s", a, 0, E // 2)
+            inverse_root(a + 1)
+            scale_rows("s", a, E // 2, E)
         inverse_root(3)
+        scale_rows("s", 2, 0, EARLY2)
+        for a in (3, 4, 5):
+            if a < 5:
+                inverse_root(a + 1)
+            scale_rows("s", a, 0, PAIR)
         nc.scalar.activation(
             out=hr[-3][:, 6:8, :].rearrange("p a e -> p (a e)").bitcast(BF16)[:, 0 : E - CUT7],
             in_=h_raw[7][:, CUT7:],
@@ -185,19 +188,17 @@ def tile_hypergraphgpslayer_pb_t_kernel(
         nc.scalar.activation(
             out=rs[:], in_=de[:], func=ACT.Abs_reciprocal_sqrt, bias=tiny[:, 0:1]
         )
-        for a in range(4, 7):
-            inverse_root(a)
+        inverse_root(6)
         inverse_root(7, dv[:, 8:9])
-        for a in (3, 4, 5, 6, 7):
+        for a in (6, 7):
             scale_rows("s", a, 0, PAIR)
 
         gbr_b = const.tile([P, DIM], F32)
         gbr = const.tile([P, 4], F32)
 
         def scale_pair(p):
-            c0 = p * PAIR
-            for a in range(4, PLANES):
-                scale_rows("g" if a > G_FROM(p) else "s", a, c0, c0 + PAIR)
+            for a in range(3, PLANES):
+                scale_rows("s", a, p * PAIR, (p + 1) * PAIR)
 
         def bias_row():
             nc.gpsimd.tensor_scalar(
@@ -218,11 +219,24 @@ def tile_hypergraphgpslayer_pb_t_kernel(
             nc.scalar.copy(out=gbr[:], in_=turned[:, :, 0])
 
         x0g = ha.tile([P, 2, DIM, 4], BF16, tag="big", align_bytes=64)
-        for g in range(2):
-            nc.vector.tensor_copy(
-                out=x0g[:, g].rearrange("p (t m) j -> p m j t", t=4),
-                in_=x0raw[:, g].rearrange("p j (m t) -> p m j t", t=4),
+        def regrouped(g):
+            return (
+                x0g[:, g].rearrange("p (t m) j -> p m j t", t=4),
+                x0raw[:, g].rearrange("p j (m t) -> p m j t", t=4),
             )
+
+        dst, src = regrouped(0)
+        nc.vector.tensor_copy(out=dst, in_=src)
+        seen_x0 = const.tile([P, 1], BF16)
+        nc.gpsimd.tensor_copy(out=seen_x0[:], in_=x0g[:, 0, 0, 0:1])
+        nc.gpsimd.tensor_scalar(
+            out=x0g[:, 1].rearrange("p (t m) j -> p t m j", t=4),
+            in0=x0raw[:, 1].rearrange("p j (m t) -> p t m j", t=4),
+            scalar1=1.0,
+            scalar2=0.0,
+            op0=ALU.mult,
+            op1=ALU.add,
+        )
         x0c = const.tile([P, 2, DIM], U32, align_bytes=64)
         x0s = const.tile([P, 2, DIM], U8, align_bytes=64)
         wc = const.tile([P, DIM], U32, align_bytes=64)
@@ -236,7 +250,7 @@ def tile_hypergraphgpslayer_pb_t_kernel(
             )
 
         def regroup_w():
-            nc.vector.tensor_copy(
+            nc.scalar.copy(
                 out=wst[:, 1].rearrange("p (c i t) -> p c t i", i=4, t=4),
                 in_=wst[:, 0].rearrange("p (t c i) -> p c t i", i=4, t=4),
             )
@@ -249,7 +263,10 @@ def tile_hypergraphgpslayer_pb_t_kernel(
         x1_tiles, spreads, groups, codes, rets, ret_codes, ys, obs = {}, {}, {}, {}, {}, {}, {}, {}
 
         def load_x1(p):
-            x1t = x1_pool.tile([P, PAIR // P, DIM], BF16, tag="x1")
+            if p == PAIRS - 1:
+                x1t = hb.tile([P, PAIR // P, DIM], BF16, tag="big", align_bytes=64)
+            else:
+                x1t = x1_pool.tile([P, PAIR // P, DIM], BF16, tag="x1")
             nc.sync.dma_start(
                 out=x1t[:],
                 in_=x_1_new[p * PAIR : (p + 1) * PAIR, :].rearrange("(s m) o -> m s o", m=P),
@@ -388,7 +405,7 @@ def tile_hypergraphgpslayer_pb_t_kernel(
                         op1=ALU.add,
                     )
 
-        held, to_store = [], []
+        held, to_store, direct_banks = [], [], {}
 
         def store(e0, n):
             p, d0 = divmod(e0, PAIR)
@@ -396,6 +413,40 @@ def tile_hypergraphgpslayer_pb_t_kernel(
                 out=out[e0 : e0 + n, :].rearrange("(s m) o -> m s o", m=P),
                 in_=obs[p][:, d0 // P : (d0 + n) // P, :],
             )
+
+        def residual_bias(k):
+            p, row = out_rows(k, 0)
+            if p not in obs:
+                obs[p] = hr_pool.tile([P, PAIR // P, DIM], F32, tag="hr", name="ob")
+            nc.gpsimd.tensor_tensor(
+                out=obs[p][:, row, :], in0=x1_tiles[p][:, row, :], in1=gbr_b[:], op=ALU.add
+            )
+
+        def direct(k):
+            rc, rsc = ret_codes[k]
+            upd = pb.tile([P, 2 * CH], F32, tag="b", name="upd")
+            nc.tensor.matmul_mx(
+                out=upd[:],
+                lhsT=rc[:, 0:P].bitcast(FP8X4),
+                lhsT_scale=rsc[:, 0:P],
+                rhs=wc[:].bitcast(FP8X4),
+                rhs_scale=ws[:],
+                start=True,
+                stop=True,
+            )
+            direct_banks[k] = upd
+
+        def add_direct(k):
+            p, row = out_rows(k, 0)
+            nc.vector.scalar_tensor_tensor(
+                out=obs[p][:, row, :],
+                in0=direct_banks[k][:],
+                scalar=g_col[:, 0:1],
+                in1=obs[p][:, row, :],
+                op0=ALU.mult,
+                op1=ALU.add,
+            )
+            store(starts[k], P)
 
         def finish(k):
             n, z_out = ROUND_PLAN[k][0], ROUND_PLAN[k][3]
@@ -434,8 +485,8 @@ def tile_hypergraphgpslayer_pb_t_kernel(
                 to_store.append((starts[k], n))
             elif (starts[k] + n) % PAIR == 0:
                 to_store.append((p * PAIR, PAIR))
-                if p + 3 < PAIRS:
-                    load_x1(p + 3)
+                if p + 2 < PAIRS - 1:
+                    load_x1(p + 2)
             if not held:
                 empty_held()
 
@@ -451,62 +502,70 @@ def tile_hypergraphgpslayer_pb_t_kernel(
             seen = const.tile([P, 1], U32, tag="seen")
             nc.gpsimd.tensor_copy(out=seen[:], in_=codes[k][0][:, 0:1])
 
+        late = [(a, p) for p in range(2, PAIRS) for a in range(3, PLANES) if (a, p) not in BY_S]
+
         def late_scale(k):
-            p = k // 2 + 2
-            if p < PAIRS:
-                for a, engine in LATE[k % 2]:
-                    scale_rows(engine, a, p * PAIR, (p + 1) * PAIR)
+            if k >= 1:
+                for a, p in late[2 * (k - 1) : 2 * k]:
+                    scale_rows("g", a, p * PAIR, (p + 1) * PAIR)
+            if k in (5, 7, 9, 11):
+                a, p = BY_S[(k - 5) // 2]
+                scale_rows("s", a, p * PAIR, (p + 1) * PAIR)
 
         def update_both(k):
             update(k, 0)
             update(k, 1)
 
-        for p in range(3):
+        for p in range(2):
             load_x1(p)
         spread(0)
+        def is_direct(k):
+            return ROUND_PLAN[k][0] == P
+
+        last = n_rounds - 1
         for k in range(n_rounds):
             normalise(k)
             empty_held()
+            if k >= 3 and is_direct(k - 3):
+                direct(k - 3)
+                add_direct(k - 3)
             if k == 0:
-                scale_rows("s", 3, PAIR, E)
+                scale_rows("s", 2, EARLY2, E)
                 scale_pair(1)
-                scale_rows("s", 2, 3072, E)
-                bias_row()
             else:
                 pace(k - 1)
+            if k == 2:
+                bias_row()
+            if is_direct(k):
+                residual_bias(k)
             late_scale(k)
+            if k == 13:
+                load_x1(PAIRS - 1)
             if k + 1 < n_rounds and starts[k + 1] % PAIR == 0:
                 spread(starts[k + 1] // PAIR)
             if k >= 1:
                 messages(k - 1, 0)
                 messages(k - 1, 1)
-            if k >= 3:
+            if k >= 3 and not is_direct(k - 3):
                 update_both(k - 3)
-            if k >= 4:
+            if k >= 4 and not is_direct(k - 4):
                 finish(k - 4)
             if k == 0:
                 quantise_x0()
-            if k == 1:
+            if k == 2:
                 quantise_w()
             if k >= 2:
                 quantise_ret(k - 2)
             quantise_h(k)
             if k == 0:
                 regroup_w()
-        last = n_rounds - 1
+        messages(last, 0)
+        direct(last - 2)
         empty_held()
-        for h in range(2):
-            messages(last, h)
         quantise_ret(last - 1)
-        update_both(last - 2)
-        finish(last - 3)
+        direct(last - 1)
+        add_direct(last - 2)
         quantise_ret(last)
-        empty_held()
-        update_both(last - 1)
-        finish(last - 2)
-        empty_held()
-        update_both(last)
-        finish(last - 1)
-        empty_held()
-        finish(last)
-        empty_held()
+        direct(last)
+        add_direct(last - 1)
+        add_direct(last)

@@ -23,15 +23,16 @@ CH = 256
 PAIR = 512
 PAIRS = E // PAIR
 TINY = 1e-20
-EARLY2 = 1536
-BY_S = ((7, 4), (7, 5), (7, 6), (7, 7))
+EARLY2 = 512
+BY_S = ((7, 3), (7, 4), (7, 5), (7, 6), (7, 7))
 
 
-CUT7 = 2560
+CUT = 3072
 
 ROUND_PLAN = (
-    [(256, "ss", "ssss", "ss"), (256, "ss", "ssss", "ss"), (256, "ss", "ssss", "sv")] * 4
-    + [(256, "ss", "ssss", "sv")] * 2
+    [(256, "ss", "ssss", "ss")] * 3
+    + [(256, "ss", "ssss", "sv"), (256, "ss", "ssss", "ss"), (256, "ss", "ssss", "ss")] * 2
+    + [(256, "ss", "ssss", "sv")] * 5
     + [(128, "s", "ssss", "s")] * 4
 )
 
@@ -65,16 +66,18 @@ def tile_hypergraphgpslayer_pb_t_kernel(
         for a in range(PLANES):
             pool = ha if a < 4 else hb
             h_a = pool.tile([P, E], BF16, tag="big", align_bytes=64, name="h_a")
-            cuts = [(0, E)] if a < PLANES - 1 else [(0, CUT7), (CUT7, E - CUT7)]
+            cuts = [(0, E)] if a < PLANES - 1 else [(0, CUT), (CUT, E - CUT)]
             for c0, n in cuts:
                 nc.sync.dma_start(out=h_a[:, c0 : c0 + n], in_=h_dram[:, a // 4, a % 4, c0 : c0 + n])
                 pieces.append((a, c0, n))
             h_raw.append(h_a)
 
         x0raw = ha.tile([P, 2, 4, DIM], BF16, tag="big", align_bytes=64)
-        nc.sync.dma_start(
-            out=x0raw[:], in_=x_0_local.rearrange("(g p j) d -> p g j d", g=2, j=4)
-        )
+        for g in range(2):
+            nc.sync.dma_start(
+                out=x0raw[:, g],
+                in_=x_0_local.rearrange("(g p j) d -> p g j d", g=2, j=4)[:, g],
+            )
         wst = ha.tile([P, 2, 4 * DIM], BF16, tag="big", align_bytes=64)
         wraw = wst[:, 0].rearrange("p (t o) -> p t o", t=4)
         nc.sync.dma_start(out=wraw, in_=Wr.rearrange("(p t) o -> p t o", t=4))
@@ -109,7 +112,7 @@ def tile_hypergraphgpslayer_pb_t_kernel(
             )
         )
 
-        dv = const.tile([P, PLANES + 1], F32)
+        dv = const.tile([P, PLANES + 2], F32)
         rv = const.tile([P, PLANES], F32)
         hr = [hr_pool.tile([P, PLANES, PAIR], F32, tag="hr", name="hr_p") for p in range(PAIRS)]
         dep = pc.tile([P, PLANES, E // P], F32, tag="c")
@@ -127,6 +130,15 @@ def tile_hypergraphgpslayer_pb_t_kernel(
                 in1=h_raw[a][:, c0 + half : c0 + n],
                 op0=ALU.add,
                 op1=ALU.add,
+                accum_out=dv[:, slot : slot + 1],
+            )
+
+        def scalar_row_sums(a, slot):
+            unread_s = hr[-3][:, 2 * a - 8 : 2 * a - 6, :].rearrange("p a e -> p (a e)")
+            nc.scalar.activation(
+                out=unread_s.bitcast(BF16)[:, 0 : E - CUT],
+                in_=h_raw[a][:, CUT:],
+                func=ACT.Copy,
                 accum_out=dv[:, slot : slot + 1],
             )
 
@@ -159,9 +171,8 @@ def tile_hypergraphgpslayer_pb_t_kernel(
                     stop=True,
                 )
 
-        for a in range(PLANES - 1):
-            row_sums(a, 0, E, a)
-        row_sums(7, 0, CUT7, 7)
+        for a in range(PLANES):
+            row_sums(a, 0, E if a < 6 else CUT, a)
         de = const.tile([P, E // P], F32)
         nc.vector.tensor_reduce(
             out=de[:], in_=dep[:].rearrange("p a c -> p c a"), axis=AX.X, op=ALU.add
@@ -176,19 +187,18 @@ def tile_hypergraphgpslayer_pb_t_kernel(
         inverse_root(3)
         scale_rows("s", 2, 0, EARLY2)
         for a in (3, 4, 5):
-            if a < 5:
-                inverse_root(a + 1)
+            if a == 3:
+                inverse_root(4)
+            if a == 5:
+                scalar_row_sums(6, 9)
             scale_rows("s", a, 0, PAIR)
-        nc.scalar.activation(
-            out=hr[-3][:, 6:8, :].rearrange("p a e -> p (a e)").bitcast(BF16)[:, 0 : E - CUT7],
-            in_=h_raw[7][:, CUT7:],
-            func=ACT.Copy,
-            accum_out=dv[:, 8:9],
-        )
+            if a == 4:
+                inverse_root(5)
+        scalar_row_sums(7, 8)
         nc.scalar.activation(
             out=rs[:], in_=de[:], func=ACT.Abs_reciprocal_sqrt, bias=tiny[:, 0:1]
         )
-        inverse_root(6)
+        inverse_root(6, dv[:, 9:10])
         inverse_root(7, dv[:, 8:9])
         for a in (6, 7):
             scale_rows("s", a, 0, PAIR)
@@ -209,6 +219,8 @@ def tile_hypergraphgpslayer_pb_t_kernel(
                 op0=ALU.mult,
                 op1=ALU.add,
             )
+
+        def bias_column():
             turned = pb.tile([P, 4, P], F32, tag="b")
             for q in range(4):
                 nc.tensor.transpose(
@@ -264,7 +276,7 @@ def tile_hypergraphgpslayer_pb_t_kernel(
 
         def load_x1(p):
             if p == PAIRS - 1:
-                x1t = hb.tile([P, PAIR // P, DIM], BF16, tag="big", align_bytes=64)
+                x1t = ha.tile([P, PAIR // P, DIM], BF16, tag="big", align_bytes=64)
             else:
                 x1t = x1_pool.tile([P, PAIR // P, DIM], BF16, tag="x1")
             nc.sync.dma_start(
@@ -505,11 +517,10 @@ def tile_hypergraphgpslayer_pb_t_kernel(
         late = [(a, p) for p in range(2, PAIRS) for a in range(3, PLANES) if (a, p) not in BY_S]
 
         def late_scale(k):
-            if k >= 1:
-                for a, p in late[2 * (k - 1) : 2 * k]:
-                    scale_rows("g", a, p * PAIR, (p + 1) * PAIR)
-            if k in (5, 7, 9, 11):
-                a, p = BY_S[(k - 5) // 2]
+            for a, p in late[max(2 * k - 3, 0) : max(2 * k - 1, 0)]:
+                scale_rows("g", a, p * PAIR, (p + 1) * PAIR)
+            if k in (3, 5, 7, 9, 11):
+                a, p = BY_S[(k - 3) // 2]
                 scale_rows("s", a, p * PAIR, (p + 1) * PAIR)
 
         def update_both(k):
@@ -534,18 +545,20 @@ def tile_hypergraphgpslayer_pb_t_kernel(
                 scale_pair(1)
             else:
                 pace(k - 1)
-            if k == 2:
+            if k == 1:
                 bias_row()
             if is_direct(k):
                 residual_bias(k)
             late_scale(k)
-            if k == 13:
+            if k == 11:
                 load_x1(PAIRS - 1)
             if k + 1 < n_rounds and starts[k + 1] % PAIR == 0:
                 spread(starts[k + 1] // PAIR)
             if k >= 1:
                 messages(k - 1, 0)
                 messages(k - 1, 1)
+            if k == 2:
+                bias_column()
             if k >= 3 and not is_direct(k - 3):
                 update_both(k - 3)
             if k >= 4 and not is_direct(k - 4):

from contextlib import ExitStack

import concourse.bass as bass
import concourse.mybir as mybir
import concourse.tile as tile
from concourse.masks import make_identity

F32 = mybir.dt.float32
BF16 = mybir.dt.bfloat16
U32 = mybir.dt.uint32
U8 = mybir.dt.uint8
FP8X4 = mybir.dt.float8_e4m3fn_x4
ALU = mybir.AluOpType
ACT = mybir.ActivationFunctionType
AX = mybir.AxisListType

P = 128
N_NODES = 1024
E = 4096
DIM = 512
PLANES = 8
CH = 256
PAIR = 512
PAIRS = E // PAIR
TINY = 1e-20
EARLY2 = 512
BY_S = ((7, 3), (7, 4), (7, 5), (7, 6), (7, 7))


CUT = 3072

ROUND_PLAN = (
    [(256, "ss", "ssss", "ss")] * 3
    + [(256, "ss", "ssss", "sv"), (256, "ss", "ssss", "ss"), (256, "ss", "ssss", "ss")] * 2
    + [(256, "ss", "ssss", "sv")] * 5
    + [(128, "s", "ssss", "s")] * 4
)


FLOPS = 2 * E * N_NODES * DIM + 2 * E * DIM * DIM


def tile_hypergraphgpslayer_pb_t_kernel(
    tc, x_0_local, x_1_new, incidence_1, Wr, br, gate_return, out
):
    nc = tc.nc
    with ExitStack() as ctx:
        const = ctx.enter_context(tc.tile_pool(name="const", bufs=1))
        hr_pool = ctx.enter_context(tc.tile_pool(name="hr", bufs=PAIRS))
        ha = ctx.enter_context(tc.tile_pool(name="ha", bufs=6))
        hb = ctx.enter_context(tc.tile_pool(name="hb", bufs=4))
        hq_pool = ctx.enter_context(tc.tile_pool(name="hq", bufs=2))
        rg_pool = ctx.enter_context(tc.tile_pool(name="rg", bufs=2))
        x1_pool = ctx.enter_context(tc.tile_pool(name="x1", bufs=2))
        ps = ctx.enter_context(tc.psum_pool(name="ps", bufs=2))
        pa = ctx.enter_context(tc.psum_pool(name="pa", bufs=2))
        pb = ctx.enter_context(tc.psum_pool(name="pb", bufs=2))
        pc = ctx.enter_context(tc.psum_pool(name="pc", bufs=2))

        gate_b = const.tile([P, 1], BF16)
        nc.scalar.dma_start(out=gate_b[:], in_=gate_return.partition_broadcast(P))

        h_dram = incidence_1.rearrange("(g p j) e -> p g j e", g=2, j=4)
        h_raw = []
        pieces = []
        for a in range(PLANES):
            pool = ha if a < 4 else hb
            h_a = pool.tile([P, E], BF16, tag="big", align_bytes=64, name="h_a")
            cuts = [(0, E)] if a < PLANES - 1 else [(0, CUT), (CUT, E - CUT)]
            for c0, n in cuts:
                nc.sync.dma_start(out=h_a[:, c0 : c0 + n], in_=h_dram[:, a // 4, a % 4, c0 : c0 + n])
                pieces.append((a, c0, n))
            h_raw.append(h_a)

        x0raw = ha.tile([P, 2, 4, DIM], BF16, tag="big", align_bytes=64)
        for g in range(2):
            nc.sync.dma_start(
                out=x0raw[:, g],
                in_=x_0_local.rearrange("(g p j) d -> p g j d", g=2, j=4)[:, g],
            )
        wst = ha.tile([P, 2, 4 * DIM], BF16, tag="big", align_bytes=64)
        wraw = wst[:, 0].rearrange("p (t o) -> p t o", t=4)
        nc.sync.dma_start(out=wraw, in_=Wr.rearrange("(p t) o -> p t o", t=4))

        br_b = rg_pool.tile([P, DIM], BF16, tag="rg", align_bytes=64)
        nc.sync.dma_start(out=br_b[:], in_=br.partition_broadcast(P))

        ident = const.tile([P, P], F32)
        make_identity(nc, ident[:])
        ident_bf = const.tile([P, P], BF16)
        nc.vector.tensor_copy(out=ident_bf[:], in_=ident[:])
        ones = const.tile([P, 2], BF16)
        nc.vector.memset(ones[:], 1.0)
        tiny = const.tile([P, 1], F32)
        nc.vector.memset(tiny[:], TINY)

        g_col = const.tile([P, 1], F32)
        nc.scalar.activation(out=g_col[:], in_=gate_b[:], func=ACT.Tanh)
        warm = const.tile([P, 1], F32)
        nc.scalar.activation(
            out=warm[:], in_=g_col[:], func=ACT.Abs_reciprocal_sqrt, bias=1.0, scale=0.0
        )

        ctx.enter_context(
            tc.manual_schedule(
                engines={
                    mybir.EngineType.DVE,
                    mybir.EngineType.Activation,
                    mybir.EngineType.PE,
                    mybir.EngineType.Pool,
                }
            )
        )

        dv = const.tile([P, PLANES + 2], F32)
        rv = const.tile([P, PLANES], F32)
        hr = [hr_pool.tile([P, PLANES, PAIR], F32, tag="hr", name="hr_p") for p in range(PAIRS)]
        dep = pc.tile([P, PLANES, E // P], F32, tag="c")

        def unread(a):
            two = a - a % 2
            return hr[a % 2 - 2][:, two : two + 2, :].rearrange("p a e -> p (a e)").bitcast(BF16)

        def row_sums(a, c0, n, slot):
            half = n // 2
            nc.vector.scalar_tensor_tensor(
                out=unread(a)[:, 0:half],
                in0=h_raw[a][:, c0 : c0 + half],
                scalar=TINY,
                in1=h_raw[a][:, c0 + half : c0 + n],
                op0=ALU.add,
                op1=ALU.add,
                accum_out=dv[:, slot : slot + 1],
            )

        def scalar_row_sums(a, slot):
            unread_s = hr[-3][:, 2 * a - 8 : 2 * a - 6, :].rearrange("p a e -> p (a e)")
            nc.scalar.activation(
                out=unread_s.bitcast(BF16)[:, 0 : E - CUT],
                in_=h_raw[a][:, CUT:],
                func=ACT.Copy,
                accum_out=dv[:, slot : slot + 1],
            )

        def inverse_root(a, bias=0.0):
            nc.scalar.activation(
                out=rv[:, a : a + 1], in_=dv[:, a : a + 1], func=ACT.Abs_reciprocal_sqrt, bias=bias
            )

        def scale_rows(engine, a, c0, c1):
            step = PAIR
            for c in range(c0, c1, step):
                dst = hr[c // PAIR][:, a, c % PAIR : c % PAIR + step]
                src, by = h_raw[a][:, c : c + step], rv[:, a : a + 1]
                if engine == "s":
                    nc.scalar.activation(out=dst, in_=src, func=ACT.Copy, scale=by)
                elif engine == "v":
                    nc.vector.tensor_scalar_mul(out=dst, in0=src, scalar1=by)
                else:
                    nc.gpsimd.tensor_scalar(
                        out=dst, in0=src, scalar1=by, scalar2=0.0, op0=ALU.mult, op1=ALU.add
                    )

        for a, c0, n in pieces:
            for c in range(c0 // P, (c0 + n) // P):
                nc.tensor.matmul(
                    out=dep[:, a, c : c + 1],
                    lhsT=h_raw[a][:, c * P : (c + 1) * P],
                    rhs=ones[:, 0:1],
                    start=True,
                    stop=True,
                )

        for a in range(PLANES):
            row_sums(a, 0, E if a < 6 else CUT, a)
        de = const.tile([P, E // P], F32)
        nc.vector.tensor_reduce(
            out=de[:], in_=dep[:].rearrange("p a c -> p c a"), axis=AX.X, op=ALU.add
        )
        rs = const.tile([P, E // P], F32)

        inverse_root(0)
        for a in range(2):
            scale_rows("s", a, 0, E // 2)
            inverse_root(a + 1)
            scale_rows("s", a, E // 2, E)
        inverse_root(3)
        scale_rows("s", 2, 0, EARLY2)
        for a in (3, 4, 5):
            if a == 3:
                inverse_root(4)
            if a == 5:
                scalar_row_sums(6, 9)
            scale_rows("s", a, 0, PAIR)
            if a == 4:
                inverse_root(5)
        scalar_row_sums(7, 8)
        nc.scalar.activation(
            out=rs[:], in_=de[:], func=ACT.Abs_reciprocal_sqrt, bias=tiny[:, 0:1]
        )
        inverse_root(6, dv[:, 9:10])
        inverse_root(7, dv[:, 8:9])
        for a in (6, 7):
            scale_rows("s", a, 0, PAIR)

        gbr_b = const.tile([P, DIM], F32)
        gbr = const.tile([P, 4], F32)

        def scale_pair(p):
            for a in range(3, PLANES):
                scale_rows("s", a, p * PAIR, (p + 1) * PAIR)

        def bias_row():
            nc.gpsimd.tensor_scalar(
                out=gbr_b[:],
                in0=br_b[:],
                scalar1=g_col[:, 0:1],
                scalar2=0.0,
                op0=ALU.mult,
                op1=ALU.add,
            )

        def bias_column():
            turned = pb.tile([P, 4, P], F32, tag="b")
            for q in range(4):
                nc.tensor.transpose(
                    out=turned[:, q, :],
                    in_=gbr_b[:, q * P : (q + 1) * P],
                    identity=ident[:],
                )
            nc.scalar.copy(out=gbr[:], in_=turned[:, :, 0])

        x0g = ha.tile([P, 2, DIM, 4], BF16, tag="big", align_bytes=64)
        def regrouped(g):
            return (
                x0g[:, g].rearrange("p (t m) j -> p m j t", t=4),
                x0raw[:, g].rearrange("p j (m t) -> p m j t", t=4),
            )

        dst, src = regrouped(0)
        nc.vector.tensor_copy(out=dst, in_=src)
        seen_x0 = const.tile([P, 1], BF16)
        nc.gpsimd.tensor_copy(out=seen_x0[:], in_=x0g[:, 0, 0, 0:1])
        nc.gpsimd.tensor_scalar(
            out=x0g[:, 1].rearrange("p (t m) j -> p t m j", t=4),
            in0=x0raw[:, 1].rearrange("p j (m t) -> p t m j", t=4),
            scalar1=1.0,
            scalar2=0.0,
            op0=ALU.mult,
            op1=ALU.add,
        )
        x0c = const.tile([P, 2, DIM], U32, align_bytes=64)
        x0s = const.tile([P, 2, DIM], U8, align_bytes=64)
        wc = const.tile([P, DIM], U32, align_bytes=64)
        ws = const.tile([P, DIM], U8, align_bytes=64)

        def quantise_x0():
            nc.vector.quantize_mx(
                out=x0c[:].rearrange("p g c -> p (g c)").bitcast(FP8X4),
                scales=x0s[:].rearrange("p g c -> p (g c)"),
                in_=x0g[:].rearrange("p g c j -> p (g c j)"),
            )

        def regroup_w():
            nc.scalar.copy(
                out=wst[:, 1].rearrange("p (c i t) -> p c t i", i=4, t=4),
                in_=wst[:, 0].rearrange("p (t c i) -> p c t i", i=4, t=4),
            )

        def quantise_w():
            nc.vector.quantize_mx(out=wc[:].bitcast(FP8X4), scales=ws[:], in_=wst[:, 1])

        starts = [sum(plan[0] for plan in ROUND_PLAN[:k]) for k in range(len(ROUND_PLAN))]
        n_rounds = len(ROUND_PLAN)
        x1_tiles, spreads, groups, codes, rets, ret_codes, ys, obs = {}, {}, {}, {}, {}, {}, {}, {}

        def load_x1(p):
            if p == PAIRS - 1:
                x1t = ha.tile([P, PAIR // P, DIM], BF16, tag="big", align_bytes=64)
            else:
                x1t = x1_pool.tile([P, PAIR // P, DIM], BF16, tag="x1")
            nc.sync.dma_start(
                out=x1t[:],
                in_=x_1_new[p * PAIR : (p + 1) * PAIR, :].rearrange("(s m) o -> m s o", m=P),
            )
            x1_tiles[p] = x1t

        def leave_psum(engine, dst, src):
            if engine == "s":
                nc.scalar.copy(out=dst, in_=src)
            else:
                nc.vector.tensor_copy(out=dst, in_=src)

        def spread(p):
            sp = ps.tile([P, PAIR], F32, tag="s")
            for q in range(PAIR // P):
                c = p * PAIR // P + q
                nc.tensor.transpose(
                    out=sp[:, q * P : (q + 1) * P],
                    in_=rs[:, c : c + 1].to_broadcast([P, P]),
                    identity=ident[:],
                )
            spreads[p] = sp

        def normalise(k):
            n = ROUND_PLAN[k][0]
            p, d0 = divmod(starts[k], PAIR)
            hg = ha.tile([P, 2 * CH * 4], BF16, tag="big", align_bytes=64)
            hgv = hg[:, 0 : 8 * n].rearrange("p (g c i t) -> p g c t i", g=2, i=2, t=4)
            by = (
                spreads[p][:, d0 : d0 + n]
                .rearrange("p (c i) -> p c i", i=2)
                .unsqueeze(2)
                .to_broadcast([P, n // 2, 4, 2])
            )
            for g in range(2):
                nc.vector.tensor_tensor(
                    out=hgv[:, g],
                    in0=hr[p][:, 4 * g : 4 * g + 4, d0 : d0 + n].rearrange(
                        "p t (c i) -> p c t i", i=2
                    ),
                    in1=by,
                    op=ALU.mult,
                )
            groups[k] = hg

        def quantise_h(k):
            n = ROUND_PLAN[k][0]
            hc = hq_pool.tile([P, 2 * CH], U32, tag="hc", align_bytes=64)
            hs = hq_pool.tile([P, 2 * CH], U8, tag="hs", align_bytes=64)
            nc.vector.quantize_mx(
                out=hc[:, 0 : 2 * n].bitcast(FP8X4),
                scales=hs[:, 0 : 2 * n],
                in_=groups[k][:, 0 : 8 * n],
            )
            codes[k] = (hc, hs)

        def in_half(h, count):
            return range((count + 1) // 2) if h == 0 else range((count + 1) // 2, count)

        def messages(k, h):
            n, ret_out = ROUND_PLAN[k][0], ROUND_PLAN[k][1]
            hc, hs = codes[k]
            if h == 0:
                rets[k] = rg_pool.tile([P, CH * 4], BF16, tag="rg", align_bytes=64, name="rg")
            rg = rets[k]
            for s in in_half(h, n // P):
                ret = pa.tile([P, 4, P], F32, tag="a")
                for t in range(4):
                    d_sl = slice(t * P, (t + 1) * P)
                    for g in range(2):
                        h_sl = slice(g * n + s * P, g * n + (s + 1) * P)
                        nc.tensor.matmul_mx(
                            out=ret[:, t, :],
                            lhsT=x0c[:, g, d_sl].bitcast(FP8X4),
                            lhsT_scale=x0s[:, g, d_sl],
                            rhs=hc[:, h_sl].bitcast(FP8X4),
                            rhs_scale=hs[:, h_sl],
                            start=(g == 0),
                            stop=(g == 1),
                        )
                leave_psum(
                    ret_out[s],
                    rg[:, s * 4 * P : (s + 1) * 4 * P].rearrange("p (e t) -> p e t", t=4),
                    ret[:].rearrange("p t e -> p e t"),
                )

        def quantise_ret(k):
            n = ROUND_PLAN[k][0]
            rc = rg_pool.tile([P, CH], U32, tag="rc", align_bytes=64)
            rsc = rg_pool.tile([P, CH], U8, tag="rsc", align_bytes=64)
            nc.vector.quantize_mx(
                out=rc[:, 0:n].bitcast(FP8X4), scales=rsc[:, 0:n], in_=rets[k][:, 0 : 4 * n]
            )
            ret_codes[k] = (rc, rsc)

        def out_rows(k, s):
            p, d0 = divmod(starts[k] + s * P, PAIR)
            return p, d0 // P

        def update(k, h):
            n, y_out = ROUND_PLAN[k][0], ROUND_PLAN[k][2]
            rc, rsc = ret_codes[k]
            if h == 0:
                ys[k] = ha.tile([P, 4, CH], F32, tag="big", align_bytes=64, name="y")
            y = ys[k]
            updT = pb.tile([P, 2, CH], F32, tag="b")
            for i in range(2):
                q = 2 * h + i
                o_sl = slice(q * P, (q + 1) * P)
                nc.tensor.matmul_mx(
                    out=updT[:, i, 0:n],
                    lhsT=wc[:, o_sl].bitcast(FP8X4),
                    lhsT_scale=ws[:, o_sl],
                    rhs=rc[:, 0:n].bitcast(FP8X4),
                    rhs_scale=rsc[:, 0:n],
                    start=True,
                    stop=True,
                )
            for i in range(2):
                q = 2 * h + i
                if y_out[q] == "s":
                    nc.scalar.activation(
                        out=y[:, q, 0:n],
                        in_=updT[:, i, 0:n],
                        func=ACT.Identity,
                        bias=gbr[:, q : q + 1],
                        scale=g_col[:, 0:1],
                    )
                else:
                    nc.vector.tensor_scalar(
                        out=y[:, q, 0:n],
                        in0=updT[:, i, 0:n],
                        scalar1=g_col[:, 0:1],
                        scalar2=gbr[:, q : q + 1],
                        op0=ALU.mult,
                        op1=ALU.add,
                    )

        held, to_store, direct_banks = [], [], {}

        def store(e0, n):
            p, d0 = divmod(e0, PAIR)
            nc.sync.dma_start(
                out=out[e0 : e0 + n, :].rearrange("(s m) o -> m s o", m=P),
                in_=obs[p][:, d0 // P : (d0 + n) // P, :],
            )

        def residual_bias(k):
            p, row = out_rows(k, 0)
            if p not in obs:
                obs[p] = hr_pool.tile([P, PAIR // P, DIM], F32, tag="hr", name="ob")
            nc.gpsimd.tensor_tensor(
                out=obs[p][:, row, :], in0=x1_tiles[p][:, row, :], in1=gbr_b[:], op=ALU.add
            )

        def direct(k):
            rc, rsc = ret_codes[k]
            upd = pb.tile([P, 2 * CH], F32, tag="b", name="upd")
            nc.tensor.matmul_mx(
                out=upd[:],
                lhsT=rc[:, 0:P].bitcast(FP8X4),
                lhsT_scale=rsc[:, 0:P],
                rhs=wc[:].bitcast(FP8X4),
                rhs_scale=ws[:],
                start=True,
                stop=True,
            )
            direct_banks[k] = upd

        def add_direct(k):
            p, row = out_rows(k, 0)
            nc.vector.scalar_tensor_tensor(
                out=obs[p][:, row, :],
                in0=direct_banks[k][:],
                scalar=g_col[:, 0:1],
                in1=obs[p][:, row, :],
                op0=ALU.mult,
                op1=ALU.add,
            )
            store(starts[k], P)

        def finish(k):
            n, z_out = ROUND_PLAN[k][0], ROUND_PLAN[k][3]
            p = starts[k] // PAIR
            if p not in obs:
                obs[p] = hr_pool.tile([P, PAIR // P, DIM], F32, tag="hr", name="ob")
            banks = []
            for s in range(n // P):
                p, row = out_rows(k, s)
                z = pc.tile([P, DIM], F32, tag="c")
                if z_out[s] == "s":
                    nc.tensor.matmul(
                        out=z[:],
                        lhsT=ident_bf[:],
                        rhs=x1_tiles[p][:, row, :],
                        start=True,
                        stop=False,
                    )
                banks.append(z)
            for s, z in enumerate(banks):
                p, row = out_rows(k, s)
                for q in range(4):
                    nc.tensor.matmul(
                        out=z[:, q * P : (q + 1) * P],
                        lhsT=ys[k][:, q, s * P : (s + 1) * P],
                        rhs=ident[:],
                        is_transpose=True,
                        start=(z_out[s] == "v"),
                        stop=(z_out[s] == "v" or q == 3),
                    )
                if z_out[s] == "s":
                    nc.scalar.copy(out=obs[p][:, row, :], in_=z[:])
                else:
                    held.append((obs[p][:, row, :], z[:], x1_tiles[p][:, row, :]))
            if p == PAIRS - 1:
                to_store.append((starts[k], n))
            elif (starts[k] + n) % PAIR == 0:
                to_store.append((p * PAIR, PAIR))
                if p + 2 < PAIRS - 1:
                    load_x1(p + 2)
            if not held:
                empty_held()

        def empty_held():
            for dst, src, residual in held:
                nc.vector.tensor_tensor(out=dst, in0=src, in1=residual, op=ALU.add)
            for e0, n in to_store:
                store(e0, n)
            held.clear()
            to_store.clear()

        def pace(k):
            seen = const.tile([P, 1], U32, tag="seen")
            nc.gpsimd.tensor_copy(out=seen[:], in_=codes[k][0][:, 0:1])

        late = [(a, p) for p in range(2, PAIRS) for a in range(3, PLANES) if (a, p) not in BY_S]

        def late_scale(k):
            for a, p in late[max(2 * k - 3, 0) : max(2 * k - 1, 0)]:
                scale_rows("g", a, p * PAIR, (p + 1) * PAIR)
            if k in (3, 5, 7, 9, 11):
                a, p = BY_S[(k - 3) // 2]
                scale_rows("s", a, p * PAIR, (p + 1) * PAIR)

        def update_both(k):
            update(k, 0)
            update(k, 1)

        for p in range(2):
            load_x1(p)
        spread(0)
        def is_direct(k):
            return ROUND_PLAN[k][0] == P

        last = n_rounds - 1
        for k in range(n_rounds):
            normalise(k)
            empty_held()
            if k >= 3 and is_direct(k - 3):
                direct(k - 3)
                add_direct(k - 3)
            if k == 0:
                scale_rows("s", 2, EARLY2, E)
                scale_pair(1)
            else:
                pace(k - 1)
            if k == 1:
                bias_row()
            if is_direct(k):
                residual_bias(k)
            late_scale(k)
            if k == 11:
                load_x1(PAIRS - 1)
            if k + 1 < n_rounds and starts[k + 1] % PAIR == 0:
                spread(starts[k + 1] // PAIR)
            if k >= 1:
                messages(k - 1, 0)
                messages(k - 1, 1)
            if k == 2:
                bias_column()
            if k >= 3 and not is_direct(k - 3):
                update_both(k - 3)
            if k >= 4 and not is_direct(k - 4):
                finish(k - 4)
            if k == 0:
                quantise_x0()
            if k == 2:
                quantise_w()
            if k >= 2:
                quantise_ret(k - 2)
            quantise_h(k)
            if k == 0:
                regroup_w()
        messages(last, 0)
        direct(last - 2)
        empty_held()
        quantise_ret(last - 1)
        direct(last - 1)
        add_direct(last - 2)
        quantise_ret(last)
        direct(last)
        add_direct(last - 1)
        add_direct(last)
